import numpy as np
import ml_dtypes


def mxq(x, axis, fmt="e4m3"):
    dtype, down = {"e4m3": (ml_dtypes.float8_e4m3fn, 7), "e5m2": (ml_dtypes.float8_e5m2, 14)}[fmt]
    v = np.moveaxis(np.asarray(x, np.float32).astype(ml_dtypes.bfloat16).astype(np.float64), axis, -1)
    blocks = v.reshape(v.shape[:-1] + (-1, 32))
    amax = np.abs(blocks).max(-1, keepdims=True)
    byte = np.maximum(np.where(amax > 0, np.frexp(amax)[1] - 1 + 127, 0) - down, 1)
    scale = np.exp2(byte - 127.0)
    codes = (blocks / scale).astype(np.float32).astype(dtype).astype(np.float64)
    return np.moveaxis((codes * scale).reshape(v.shape), -1, axis)


WIDE = False


def mx_kscale(k):
    if not WIDE:
        return np.ones(k)
    levels = np.array([10, -10, 5, -5, 0])
    if k % 512:
        return np.exp2(np.random.permutation(np.resize(levels, k // 32))).repeat(32)
    a = np.empty((k // 512, 16))
    for p in range(k // 512):
        a[p, :8] = np.random.permutation(np.resize(levels, 8))
        for g in range(8):
            far = levels[np.abs(levels - a[p, g]) >= 10]
            a[p, g + 8] = far[np.random.randint(len(far))]
    return np.exp2(a.ravel()).repeat(32)


BF16 = ml_dtypes.bfloat16


def bf(x):
    return np.asarray(x, np.float32).astype(BF16)


def f64(x):
    return np.asarray(x).astype(np.float64)


B, H, T, D, W = 1, 4, 4096, 128, 512
NB = T // W
C0 = 4.0


def band(i, j):
    return (j[None, :] <= i[:, None]) & ((i[:, None] - j[None, :]) < W)


def lead(x, fill):
    return np.concatenate([np.full_like(x[:, :, :1], fill), x], axis=2)


def setup_inputs():
    s = mx_kscale(W)
    s = np.tile(np.roll(s, -np.argmax(s)), NB)
    q = np.random.standard_normal((B, H, T, D)) * 1.5
    k = np.random.standard_normal((B, H, T, D))
    v = np.random.standard_normal((B, H, T, D)) * 2.0
    q[..., 0] = C0
    k[..., 0] += np.log(s) * D ** 0.5 / C0
    v = v * (s.max() / s)[:, None]
    return {"q": bf(q), "k": bf(k), "v": bf(v)}


def reference(q, k, v):
    a = np.arange(W)
    qb = f64(q).reshape(B, H, NB, W, D)
    kb = f64(k).reshape(B, H, NB, W, D)
    vq = mxq(f64(v).reshape(B, H, NB, W, D), 3, "e4m3")
    s0 = np.where(band(a, a), qb @ kb.swapaxes(-1, -2) * D ** -0.5, -np.inf)
    s1 = np.where(band(a + W, a), qb[:, :, 1:] @ kb[:, :, :-1].swapaxes(-1, -2) * D ** -0.5, -np.inf)
    m = np.maximum(s0.max(-1, keepdims=True), lead(s1.max(-1, keepdims=True), -np.inf))
    e0 = np.exp(s0 - m)
    e1 = np.exp(s1 - m[:, :, 1:])
    num = (mxq(e0, 4, "e4m3") @ vq) + lead(mxq(e1, 4, "e4m3") @ vq[:, :, :-1], 0.0)
    den = e0.sum(-1, keepdims=True) + lead(e1.sum(-1, keepdims=True), 0.0)
    return (num / den).reshape(B, H, T, D)

@@ -1,0 +1,345 @@
+from contextlib import ExitStack
+
+import concourse.mybir as mybir
+from concourse.masks import make_identity
+
+F32 = mybir.dt.float32
+BF16 = mybir.dt.bfloat16
+U32 = mybir.dt.uint32
+U8 = mybir.dt.uint8
+FP8X4 = mybir.dt.float8_e4m3fn_x4
+ALU = mybir.AluOpType
+ACTF = mybir.ActivationFunctionType
+AX = mybir.AxisListType
+
+P = 128
+H = 4
+T = 4096
+W = 512
+NB = T // W
+SUBS = W // P
+NS = T // P
+SCALE = 128.0 ** -0.5
+NEG = -(2.0 ** 80)
+FLOPS = 2 * (2 * NB - 1) * H * 2 * W * W * P
+
+L_MAX = 1
+L_EXP = 2
+L_FLIP = 3
+L_QUANT = 5
+L_MX = 6
+L_OUT = 7
+SMALL = 2
+
+
+def tile_baseattention_t_kernel(tc, q, k, v, out):
+    nc = tc.nc
+    qv = q.rearrange("b h (s p) d -> p (b h s) d", p=P)
+    kv = k.rearrange("b h (s p) d -> p (b h s) d", p=P)
+    vv = v.rearrange("b h (n p t) d -> p (b h n) t d", p=P, t=4)
+    ov = out.rearrange("b h (s p) d -> p (b h s) d", p=P)
+
+    with ExitStack() as ctx:
+        const = ctx.enter_context(tc.tile_pool(name="const", bufs=1))
+        stat = ctx.enter_context(tc.tile_pool(name="stat", bufs=4))
+        wp = ctx.enter_context(tc.tile_pool(name="wp", bufs=3))
+        vgp = ctx.enter_context(tc.tile_pool(name="vgp", bufs=2))
+        tsp = ctx.enter_context(tc.tile_pool(name="tsp", bufs=3))
+        op = ctx.enter_context(tc.tile_pool(name="op", bufs=3))
+        psum = ctx.enter_context(tc.psum_pool(name="psum", bufs=1))
+        ctx.enter_context(tc.manual_schedule())
+
+        q_raw = []
+        k_raw = []
+        v_raw = []
+        for h in range(H):
+            q_raw.append(const.tile([P, NS, P], BF16, name="q_raw%d" % h))
+            k_raw.append(const.tile([P, NS, P], BF16, name="k_raw%d" % h))
+            v_raw.append(const.tile([P, NS, P], BF16, name="v_raw%d" % h))
+
+        def load(h, a, b):
+            nc.sync.dma_start(out=q_raw[h][:, a:b, :], in_=qv[:, h * NS + a:h * NS + b, :])
+            nc.sync.dma_start(out=k_raw[h][:, a:b, :], in_=kv[:, h * NS + a:h * NS + b, :])
+            nc.sync.dma_start(out=v_raw[h][:, a:b, :].rearrange("p (n t) d -> p n t d", t=4),
+                              in_=vv[:, h * NB + a // 4:h * NB + b // 4, :, :])
+
+        load(0, 0, 8)
+        load(0, 8, 16)
+        load(0, 16, NS)
+
+        ident = const.tile([P, P], BF16, name="ident")
+        make_identity(nc, ident[:])
+        mask_f = const.tile([P, 3, P], F32, name="mask_f")
+        nc.gpsimd.memset(mask_f[:, 0:2, :], 0.0)
+        nc.gpsimd.memset(mask_f[:, 2, :], NEG)
+        nc.gpsimd.affine_select(out=mask_f[:, 0, :], in_=mask_f[:, 0, :], compare_op=ALU.is_ge, fill=NEG,
+                                base=-1, pattern=[[1, P]], channel_multiplier=-1)
+        nc.gpsimd.affine_select(out=mask_f[:, 1, :], in_=mask_f[:, 1, :], compare_op=ALU.is_ge, fill=NEG,
+                                base=0, pattern=[[-1, P]], channel_multiplier=1)
+        mask = const.tile([P, 3, P], BF16, name="mask")
+        nc.vector.tensor_copy(out=mask[:], in_=mask_f[:])
+
+        grouped = []
+        for j in range(SUBS):
+            g = const.tile([P, 2, P, 4], BF16, name="grouped%d" % j, align_bytes=64)
+            nc.vector.memset(g[:].rearrange("p a c t -> p (a c t)"), 0.0)
+            grouped.append(g)
+
+        e_bufs = []
+        for j in range(2 * SUBS):
+            e_buf = const.tile([P, 2 * W], BF16, name="e_buf%d" % j)
+            nc.gpsimd.memset(e_buf[:], 0.0)
+            e_bufs.append(e_buf)
+
+        xT = []
+        v_words = []
+        v_scales = []
+        for h in range(H):
+            xT.append(const.tile([P, 2, T], BF16, name="xT%d" % h))
+            v_words.append(const.tile([P, NB, P], U32, name="v_words%d" % h, align_bytes=64))
+            v_scales.append(const.tile([P, NB, P], U8, name="v_scales%d" % h, align_bytes=64))
+
+        s_main = [psum.tile([P, W], F32, name="s_main%d" % j) for j in range(3)]
+        s_edge = [psum.tile([P, SUBS, P], F32, name="s_edge%d" % j) for j in range(2)]
+        flipped = [psum.tile([P, 2 * SUBS, P], BF16, name="flipped%d" % j) for j in range(2)]
+        o_ps = psum.tile([P, SUBS, P], F32, name="o_ps")
+        edge_bf = [t[:].rearrange("p j c -> p (j c)").bitcast(BF16).rearrange("p (j c) -> p j c", c=P) for t in s_edge]
+
+        tiles = [(h, n, qt) for h in range(H) for n in range(NB) for qt in range(SUBS)]
+        blocks = [(h, n) for h in range(H) for n in range(NB)]
+        NT = len(tiles)
+        NBLK = len(blocks)
+        state = {}
+        bstate = {}
+        ring = {"flip": 0}
+
+        def next_flip():
+            j = ring["flip"]
+            ring["flip"] = 1 - j
+            return flipped[j]
+
+        def prep_pe(b, p_ps):
+            h, n = blocks[b]
+            for j in range(SUBS):
+                nc.tensor.transpose(p_ps[:, j, :], q_raw[h][:, n * SUBS + j, :], ident[:])
+            for j in range(SUBS):
+                nc.tensor.transpose(p_ps[:, SUBS + j, :], k_raw[h][:, n * SUBS + j, :], ident[:])
+            bstate[("p", b)] = p_ps
+
+        def prep_copy(b):
+            h, n = blocks[b]
+            p_ps = bstate[("p", b)]
+            nc.vector.tensor_copy(out=xT[h][:, :, n * W:(n + 1) * W],
+                                  in_=p_ps.rearrange("p (a j) c -> p a (j c)", a=2))
+
+        def prep_v(b):
+            h, n = blocks[b]
+            v_g = vgp.tile([P, P, 4], BF16, name="v_g", align_bytes=64)
+            nc.gpsimd.tensor_scalar(out=v_g[:], in0=v_raw[h][:, n * SUBS:(n + 1) * SUBS, :].rearrange("p t d -> p d t"),
+                                    scalar1=1.0, scalar2=0.0, op0=ALU.mult, op1=ALU.add)
+            bstate[("vg", b)] = v_g
+
+        def quant_v(b):
+            h, n = blocks[b]
+            v_g = bstate[("vg", b)]
+            nc.vector.quantize_mx(out=v_words[h][:, n, :].bitcast(FP8X4), scales=v_scales[h][:, n, :],
+                                  in_=v_g[:].rearrange("p d t -> p (d t)"))
+
+        def edge_pe(b):
+            h, n = blocks[b]
+            se = s_edge[b % 2]
+            for j in range(SUBS):
+                row = n * SUBS + j
+                nc.tensor.matmul(se[:, j, :], lhsT=ident[:], rhs=mask[:, 1, :], start=True, stop=False)
+                nc.tensor.matmul(se[:, j, :], lhsT=xT[h][:, 0, row * P:(row + 1) * P],
+                                 rhs=xT[h][:, 1, row * P:(row + 1) * P], start=False, stop=True)
+
+        def edge_max(b):
+            m_edge = stat.tile([P, SUBS], F32, name="m_edge")
+            nc.vector.tensor_reduce(out=m_edge[:], in_=s_edge[b % 2][:], axis=AX.X, op=ALU.max)
+            dn = stat.tile([P, 2, SUBS], F32, name="dn")
+            bstate[("me", b)] = m_edge
+            bstate[("dn", b)] = dn
+
+        def main_pe_first(i):
+            h, n, qt = tiles[i]
+            sm = s_main[i % 3]
+            row = n * SUBS + qt
+            qT = xT[h][:, 0, row * P:(row + 1) * P]
+            k0 = (row - SUBS) * P
+            if n > 0:
+                nc.tensor.matmul(sm[:, 0:P], lhsT=ident[:], rhs=mask[:, 0, :], start=True, stop=False)
+                nc.tensor.matmul(sm[:, 0:P], lhsT=qT, rhs=xT[h][:, 1, k0:k0 + P], start=False, stop=True)
+
+        def main_pe_rest(i):
+            h, n, qt = tiles[i]
+            sm = s_main[i % 3]
+            row = n * SUBS + qt
+            qT = xT[h][:, 0, row * P:(row + 1) * P]
+            k0 = (row - SUBS) * P
+            if n > 0:
+                nc.tensor.matmul(sm[:, P:W], lhsT=qT, rhs=xT[h][:, 1, k0 + P:k0 + W], start=True, stop=True)
+            elif qt == 0:
+                nc.tensor.matmul(sm[:, W - P:W], lhsT=ident[:], rhs=mask[:, 2, :], start=True, stop=True)
+            else:
+                nc.tensor.matmul(sm[:, W - qt * P:W], lhsT=qT, rhs=xT[h][:, 1, 0:qt * P], start=True, stop=True)
+
+        def lo_col(i):
+            h, n, qt = tiles[i]
+            if n > 0:
+                return 0
+            return W - max(qt, 1) * P
+
+        def main_max(i):
+            h, n, qt = tiles[i]
+            m_main = stat.tile([P, 1], F32, name="m_main")
+            nc.vector.tensor_reduce(out=m_main[:], in_=s_main[i % 3][:, lo_col(i):W], axis=AX.X, op=ALU.max)
+            state[("mm", i)] = m_main
+
+        def combine(i):
+            h, n, qt = tiles[i]
+            m_main = state[("mm", i)]
+            nm = stat.tile([P, 1], F32, name="nm")
+            nc.vector.tensor_scalar(out=nm[:], in0=m_main[:], scalar1=bstate[("me", i // SUBS)][:, qt:qt + 1],
+                                    scalar2=-SCALE, op0=ALU.max, op1=ALU.mult)
+            state[("nm", i)] = nm
+
+        def exps(i):
+            h, n, qt = tiles[i]
+            b = i // SUBS
+            nm = state[("nm", i)]
+            dn = bstate[("dn", b)]
+            e_sb = e_bufs[i % (2 * SUBS)]
+            lo = lo_col(i)
+            c0 = qt * P
+            nc.scalar.activation(out=e_sb[:, c0 + lo:c0 + W], in_=s_main[i % 3][:, lo:W], func=ACTF.Exp,
+                                 bias=nm[:], scale=SCALE, accum_out=dn[:, 0, qt:qt + 1])
+            nc.scalar.activation(out=e_sb[:, c0 + W:c0 + W + P], in_=s_edge[b % 2][:, qt, :], func=ACTF.Exp,
+                                 bias=nm[:], scale=SCALE, accum_out=dn[:, 1, qt:qt + 1])
+            state[("e", i)] = e_sb
+
+        def flip_pe(i):
+            h, n, qt = tiles[i]
+            e_sb = state[("e", i)]
+            t_ps = next_flip()
+            for a in range(0 if n > 0 else 1, 2):
+                for t in range(4):
+                    nc.tensor.transpose(t_ps[:, 4 * a + t, :], e_sb[:, a * W + t:(a + 1) * W:4], ident[:])
+            state[("t", i)] = t_ps
+
+        def regroup(i):
+            h, n, qt = tiles[i]
+            t_ps = state[("t", i)]
+            g = grouped[qt]
+            ra = SUBS - qt
+            passes = [(qt + 1, 1)]
+            if n > 0:
+                passes.append((ra, 0))
+            for r, a in sorted(passes):
+                if r <= SMALL:
+                    t_sb = tsp.tile([P, 4, P], BF16, name="t_sb")
+                    nc.scalar.copy(out=t_sb[:], in_=t_ps[:, 4 * a:4 * a + 4, :])
+                    nc.gpsimd.tensor_scalar(out=g[:, a, :, :], in0=t_sb[:].rearrange("p t c -> p c t"),
+                                            scalar1=1.0, scalar2=0.0, op0=ALU.mult, op1=ALU.add)
+                else:
+                    nc.scalar.copy(out=g[:, a, :, :], in_=t_ps[:, 4 * a:4 * a + 4, :].rearrange("p t c -> p c t"))
+
+        def quant(i):
+            h, n, qt = tiles[i]
+            g = grouped[qt]
+            e_words = wp.tile([P, 2 * P], U32, name="e_words", align_bytes=64)
+            e_scales = wp.tile([P, 2 * P], U8, name="e_scales", align_bytes=64)
+            a0 = 0 if n > 0 else 1
+            nc.vector.quantize_mx(out=e_words[:, a0 * P:].bitcast(FP8X4), scales=e_scales[:, a0 * P:],
+                                  in_=g[:, a0:, :, :].rearrange("p a c t -> p (a c t)"))
+            state[("w", i)] = (e_words, e_scales)
+
+        def mx(i):
+            h, n, qt = tiles[i]
+            e_words, e_scales = state[("w", i)]
+            a0 = 0 if n > 0 else 1
+            for a in range(a0, 2):
+                nc.tensor.matmul_mx(out=o_ps[:, qt, :], lhsT=e_words[:, a * P:(a + 1) * P].bitcast(FP8X4),
+                                    lhsT_scale=e_scales[:, a * P:(a + 1) * P],
+                                    rhs=v_words[h][:, n - 1 + a, :].bitcast(FP8X4),
+                                    rhs_scale=v_scales[h][:, n - 1 + a, :],
+                                    start=(a == a0), stop=(a == 1))
+
+        def den_add(b):
+            dn = bstate[("dn", b)]
+            ds = stat.tile([P, SUBS], F32, name="ds")
+            nc.vector.tensor_tensor(out=ds[:], in0=dn[:, 0, :], in1=dn[:, 1, :], op=ALU.add)
+            bstate[("ds", b)] = ds
+
+        def den_recip(b):
+            rd = stat.tile([P, SUBS], F32, name="rd")
+            nc.vector.reciprocal(out=rd[:], in_=bstate[("ds", b)][:])
+            bstate[("rd", b)] = rd
+
+        def finish(b):
+            h, n = blocks[b]
+            rd = bstate[("rd", b)]
+            o_sb = op.tile([P, SUBS, P], F32, name="o_sb")
+            nc.vector.tensor_tensor(out=o_sb[:], in0=o_ps[:], in1=rd[:].unsqueeze(2).to_broadcast([P, SUBS, P]),
+                                    op=ALU.mult)
+            r0 = h * NS + n * SUBS
+            nc.sync.dma_start(out=ov[:, r0:r0 + SUBS, :], in_=o_sb[:])
+
+        for b in range(2):
+            prep_pe(b, flipped[b][:])
+            prep_copy(b)
+            prep_v(b)
+        quant_v(0)
+        quant_v(1)
+        edge_pe(0)
+        edge_max(0)
+
+        def ok(i):
+            return 0 <= i < NT
+
+        for s in range(NT + L_OUT + SUBS):
+            ph = s % SUBS
+            i_out = s - L_OUT
+            if i_out >= SUBS - 1 and i_out % SUBS == SUBS - 1 and i_out < NT:
+                finish(i_out // SUBS)
+            if s % (NB * SUBS) in (4, 12) and s // (NB * SUBS) + 1 < H:
+                half = 0 if s % (NB * SUBS) == 4 else NS // 2
+                load(s // (NB * SUBS) + 1, half, half + NS // 2)
+            if ok(s - L_FLIP):
+                flip_pe(s - L_FLIP)
+            b_prep = s // SUBS + 2
+            if ph == 2 and b_prep < NBLK:
+                prep_pe(b_prep, edge_bf[(s // SUBS + 1) % 2])
+            if ok(s):
+                main_pe_first(s)
+            if ok(s - L_MX):
+                mx(s - L_MX)
+            if ok(s):
+                main_pe_rest(s)
+            b_edge = s // SUBS + 1
+            if ph == 3 and b_edge < NBLK:
+                edge_pe(b_edge)
+            if ok(s - L_MAX):
+                main_max(s - L_MAX)
+            if ok(s - L_QUANT):
+                quant(s - L_QUANT)
+            if ok(s - L_MAX):
+                combine(s - L_MAX)
+            if ok(s - L_EXP):
+                exps(s - L_EXP)
+            if ok(s - L_FLIP):
+                regroup(s - L_FLIP)
+            i_den = s - L_EXP - 1
+            den_due = i_den >= 0 and i_den % SUBS == SUBS - 1 and i_den < NT
+            if den_due:
+                den_add(i_den // SUBS)
+            if ph == 0 and 0 < s // SUBS < NBLK:
+                edge_max(s // SUBS)
+            if ph == 2 and b_prep < NBLK:
+                prep_copy(b_prep)
+            if ph == 3 and b_prep < NBLK:
+                prep_v(b_prep)
+            if ph == 1 and 1 < s // SUBS + 1 < NBLK:
+                quant_v(s // SUBS + 1)
+            if den_due:
+                den_recip(i_den // SUBS)

@@ -5,7 +5,7 @@ from concourse.masks import make_identity
 
 F32 = mybir.dt.float32
 BF16 = mybir.dt.bfloat16
-U32 = mybir.dt.uint32
+I32 = mybir.dt.int32
 U8 = mybir.dt.uint8
 FP8X4 = mybir.dt.float8_e4m3fn_x4
 ALU = mybir.AluOpType
@@ -19,17 +19,18 @@ W = 512
 NB = T // W
 SUBS = W // P
 NS = T // P
+Q = P // SUBS
 SCALE = 128.0 ** -0.5
 NEG = -(2.0 ** 80)
 FLOPS = 2 * (2 * NB - 1) * H * 2 * W * W * P
+VW = P + P // 4
 
 L_MAX = 1
 L_EXP = 2
 L_FLIP = 3
-L_QUANT = 5
+L_QUANT = 4
 L_MX = 6
 L_OUT = 7
-SMALL = 2
 
 
 def tile_baseattention_t_kernel(tc, q, k, v, out):
@@ -42,9 +43,10 @@ def tile_baseattention_t_kernel(tc, q, k, v, out):
     with ExitStack() as ctx:
         const = ctx.enter_context(tc.tile_pool(name="const", bufs=1))
         stat = ctx.enter_context(tc.tile_pool(name="stat", bufs=4))
+        ep = ctx.enter_context(tc.tile_pool(name="ep", bufs=3))
+        gp = ctx.enter_context(tc.tile_pool(name="gp", bufs=3))
         wp = ctx.enter_context(tc.tile_pool(name="wp", bufs=3))
         vgp = ctx.enter_context(tc.tile_pool(name="vgp", bufs=2))
-        tsp = ctx.enter_context(tc.tile_pool(name="tsp", bufs=3))
         op = ctx.enter_context(tc.tile_pool(name="op", bufs=3))
         psum = ctx.enter_context(tc.psum_pool(name="psum", bufs=1))
         ctx.enter_context(tc.manual_schedule())
@@ -55,55 +57,58 @@ def tile_baseattention_t_kernel(tc, q, k, v, out):
         for h in range(H):
             q_raw.append(const.tile([P, NS, P], BF16, name="q_raw%d" % h))
             k_raw.append(const.tile([P, NS, P], BF16, name="k_raw%d" % h))
-            v_raw.append(const.tile([P, NS, P], BF16, name="v_raw%d" % h))
+            v_raw.append(const.tile([P, NB, 4, P], BF16, name="v_raw%d" % h))
 
-        def load(h, a, b):
+        def load(h, n0, n1):
+            a = n0 * SUBS
+            b = n1 * SUBS
             nc.sync.dma_start(out=q_raw[h][:, a:b, :], in_=qv[:, h * NS + a:h * NS + b, :])
             nc.sync.dma_start(out=k_raw[h][:, a:b, :], in_=kv[:, h * NS + a:h * NS + b, :])
-            nc.sync.dma_start(out=v_raw[h][:, a:b, :].rearrange("p (n t) d -> p n t d", t=4),
-                              in_=vv[:, h * NB + a // 4:h * NB + b // 4, :, :])
+            nc.sync.dma_start(out=v_raw[h][:, n0:n1, :, :], in_=vv[:, h * NB + n0:h * NB + n1, :, :])
 
-        load(0, 0, 8)
-        load(0, 8, 16)
-        load(0, 16, NS)
+        load(0, 0, 2)
+        load(0, 2, 4)
+        load(0, 4, NB)
 
         ident = const.tile([P, P], BF16, name="ident")
         make_identity(nc, ident[:])
-        mask_f = const.tile([P, 3, P], F32, name="mask_f")
-        nc.gpsimd.memset(mask_f[:, 0:2, :], 0.0)
-        nc.gpsimd.memset(mask_f[:, 2, :], NEG)
+        ident_f = const.tile([P, P], F32, name="ident_f")
+        make_identity(nc, ident_f[:])
+        mask_f = const.tile([P, 2, P], F32, name="mask_f")
+        nc.gpsimd.memset(mask_f[:], 0.0)
         nc.gpsimd.affine_select(out=mask_f[:, 0, :], in_=mask_f[:, 0, :], compare_op=ALU.is_ge, fill=NEG,
                                 base=-1, pattern=[[1, P]], channel_multiplier=-1)
         nc.gpsimd.affine_select(out=mask_f[:, 1, :], in_=mask_f[:, 1, :], compare_op=ALU.is_ge, fill=NEG,
                                 base=0, pattern=[[-1, P]], channel_multiplier=1)
-        mask = const.tile([P, 3, P], BF16, name="mask")
-        nc.vector.tensor_copy(out=mask[:], in_=mask_f[:])
-
-        grouped = []
-        for j in range(SUBS):
-            g = const.tile([P, 2, P, 4], BF16, name="grouped%d" % j, align_bytes=64)
-            nc.vector.memset(g[:].rearrange("p a c t -> p (a c t)"), 0.0)
-            grouped.append(g)
-
-        e_bufs = []
-        for j in range(2 * SUBS):
-            e_buf = const.tile([P, 2 * W], BF16, name="e_buf%d" % j)
-            nc.gpsimd.memset(e_buf[:], 0.0)
-            e_bufs.append(e_buf)
+        mask = const.tile([P, 1 + SUBS, P], BF16, name="mask")
+        for j in range(1 + SUBS):
+            nc.vector.tensor_copy(out=mask[:, j, :], in_=mask_f[:, min(j, 1), :])
 
         xT = []
-        v_words = []
-        v_scales = []
         for h in range(H):
             xT.append(const.tile([P, 2, T], BF16, name="xT%d" % h))
-            v_words.append(const.tile([P, NB, P], U32, name="v_words%d" % h, align_bytes=64))
-            v_scales.append(const.tile([P, NB, P], U8, name="v_scales%d" % h, align_bytes=64))
+        NVQ = 6
+        NVM = 4
+        v_own = []
+        v_mix = []
+        v_diag = []
+        for j in range(NVQ):
+            t = const.tile([P, VW], I32, name="v_own%d" % j, align_bytes=64)
+            nc.gpsimd.memset(t[:], 0)
+            v_own.append(t)
+        for j in range(NVM):
+            t = const.tile([P, SUBS - 1, VW], I32, name="v_mix%d" % j, align_bytes=64)
+            v_mix.append(t)
+            u = const.tile([P, SUBS, VW], I32, name="v_diag%d" % j, align_bytes=64)
+            nc.gpsimd.memset(u[:], 0)
+            v_diag.append(u)
 
         s_main = [psum.tile([P, W], F32, name="s_main%d" % j) for j in range(3)]
         s_edge = [psum.tile([P, SUBS, P], F32, name="s_edge%d" % j) for j in range(2)]
-        flipped = [psum.tile([P, 2 * SUBS, P], BF16, name="flipped%d" % j) for j in range(2)]
+        flipped = [psum.tile([P, 4, P], F32, name="flipped%d" % j) for j in range(2)]
         o_ps = psum.tile([P, SUBS, P], F32, name="o_ps")
         edge_bf = [t[:].rearrange("p j c -> p (j c)").bitcast(BF16).rearrange("p (j c) -> p j c", c=P) for t in s_edge]
+        flip_bf = [t[:].rearrange("p j c -> p (j c)").bitcast(BF16).rearrange("p (j c) -> p j c", c=P) for t in flipped]
 
         tiles = [(h, n, qt) for h in range(H) for n in range(NB) for qt in range(SUBS)]
         blocks = [(h, n) for h in range(H) for n in range(NB)]
@@ -111,12 +116,10 @@ def tile_baseattention_t_kernel(tc, q, k, v, out):
         NBLK = len(blocks)
         state = {}
         bstate = {}
-        ring = {"flip": 0}
 
-        def next_flip():
-            j = ring["flip"]
-            ring["flip"] = 1 - j
-            return flipped[j]
+        def has_main(i):
+            h, n, qt = tiles[i]
+            return n > 0 or qt > 0
 
         def prep_pe(b, p_ps):
             h, n = blocks[b]
@@ -129,79 +132,100 @@ def tile_baseattention_t_kernel(tc, q, k, v, out):
         def prep_copy(b):
             h, n = blocks[b]
             p_ps = bstate[("p", b)]
-            nc.vector.tensor_copy(out=xT[h][:, :, n * W:(n + 1) * W],
-                                  in_=p_ps.rearrange("p (a j) c -> p a (j c)", a=2))
+            nc.scalar.copy(out=xT[h][:, :, n * W:(n + 1) * W], in_=p_ps.rearrange("p (a j) c -> p a (j c)", a=2))
 
         def prep_v(b):
             h, n = blocks[b]
             v_g = vgp.tile([P, P, 4], BF16, name="v_g", align_bytes=64)
-            nc.gpsimd.tensor_scalar(out=v_g[:], in0=v_raw[h][:, n * SUBS:(n + 1) * SUBS, :].rearrange("p t d -> p d t"),
+            nc.gpsimd.tensor_scalar(out=v_g[:], in0=v_raw[h][:, n, :, :].rearrange("p t d -> p d t"),
                                     scalar1=1.0, scalar2=0.0, op0=ALU.mult, op1=ALU.add)
             bstate[("vg", b)] = v_g
+
+        def codes(ap):
+            return ap[:, 0:P].bitcast(FP8X4)
+
+        def scales(ap):
+            return ap[:, P:VW].bitcast(U8)
 
         def quant_v(b):
             h, n = blocks[b]
             v_g = bstate[("vg", b)]
-            nc.vector.quantize_mx(out=v_words[h][:, n, :].bitcast(FP8X4), scales=v_scales[h][:, n, :],
-                                  in_=v_g[:].rearrange("p d t -> p (d t)"))
+            own = v_own[b % NVQ]
+            nc.vector.quantize_mx(out=codes(own), scales=scales(own), in_=v_g[:].rearrange("p d t -> p (d t)"))
+
+        def spread_v(b):
+            h, n = blocks[b]
+            own = v_own[b % NVQ]
+            prev = v_own[(b - 1) % NVQ]
+            mix = v_mix[b % NVM]
+            diag = v_diag[b % NVM]
+            for j in range(SUBS):
+                rows = slice(j * Q, (j + 1) * Q)
+                nc.sync.dma_start(out=diag[rows, j, :], in_=own[rows, :])
+                if n > 0:
+                    if j < SUBS - 1:
+                        r = SUBS - 1 - j
+                        nc.sync.dma_start(out=mix[rows, j:, :], in_=own[rows, :].unsqueeze(1).to_broadcast([Q, r, VW]))
+                    if j > 0:
+                        nc.sync.dma_start(out=mix[rows, 0:j, :], in_=prev[rows, :].unsqueeze(1).to_broadcast([Q, j, VW]))
 
         def edge_pe(b):
             h, n = blocks[b]
             se = s_edge[b % 2]
+            nc.tensor.matmul(se[:].rearrange("p j c -> p (j c)"), lhsT=ident[:],
+                             rhs=mask[:, 1:, :].rearrange("p j c -> p (j c)"), start=True, stop=False)
             for j in range(SUBS):
                 row = n * SUBS + j
-                nc.tensor.matmul(se[:, j, :], lhsT=ident[:], rhs=mask[:, 1, :], start=True, stop=False)
                 nc.tensor.matmul(se[:, j, :], lhsT=xT[h][:, 0, row * P:(row + 1) * P],
-                                 rhs=xT[h][:, 1, row * P:(row + 1) * P], start=False, stop=True)
+                                 rhs=xT[h][:, 1, row * P:(row + 1) * P], start=False, stop=(j == SUBS - 1))
 
         def edge_max(b):
             m_edge = stat.tile([P, SUBS], F32, name="m_edge")
             nc.vector.tensor_reduce(out=m_edge[:], in_=s_edge[b % 2][:], axis=AX.X, op=ALU.max)
             dn = stat.tile([P, 2, SUBS], F32, name="dn")
+            if blocks[b][1] == 0:
+                nc.gpsimd.memset(dn[:, 0, 0:1], 0.0)
             bstate[("me", b)] = m_edge
             bstate[("dn", b)] = dn
+            e_diag = ep.tile([P, 2, SUBS, Q, 2], BF16, name="e_diag")
+            bstate[("ed", b)] = e_diag
 
-        def main_pe_first(i):
+        def main_pe_prev(i):
             h, n, qt = tiles[i]
+            if n == 0:
+                return
             sm = s_main[i % 3]
             row = n * SUBS + qt
             qT = xT[h][:, 0, row * P:(row + 1) * P]
             k0 = (row - SUBS) * P
-            if n > 0:
-                nc.tensor.matmul(sm[:, 0:P], lhsT=ident[:], rhs=mask[:, 0, :], start=True, stop=False)
-                nc.tensor.matmul(sm[:, 0:P], lhsT=qT, rhs=xT[h][:, 1, k0:k0 + P], start=False, stop=True)
+            nc.tensor.matmul(sm[:, qt * P:W], lhsT=qT, rhs=xT[h][:, 1, k0:n * W], start=True, stop=False)
+            nc.tensor.matmul(sm[:, qt * P:(qt + 1) * P], lhsT=ident[:], rhs=mask[:, 0, :], start=False, stop=True)
 
-        def main_pe_rest(i):
+        def main_pe_own(i):
             h, n, qt = tiles[i]
+            if qt == 0:
+                return
             sm = s_main[i % 3]
             row = n * SUBS + qt
             qT = xT[h][:, 0, row * P:(row + 1) * P]
-            k0 = (row - SUBS) * P
-            if n > 0:
-                nc.tensor.matmul(sm[:, P:W], lhsT=qT, rhs=xT[h][:, 1, k0 + P:k0 + W], start=True, stop=True)
-            elif qt == 0:
-                nc.tensor.matmul(sm[:, W - P:W], lhsT=ident[:], rhs=mask[:, 2, :], start=True, stop=True)
-            else:
-                nc.tensor.matmul(sm[:, W - qt * P:W], lhsT=qT, rhs=xT[h][:, 1, 0:qt * P], start=True, stop=True)
+            nc.tensor.matmul(sm[:, 0:qt * P], lhsT=qT, rhs=xT[h][:, 1, n * W:row * P], start=True, stop=True)
 
-        def lo_col(i):
+        def live(i):
             h, n, qt = tiles[i]
-            if n > 0:
-                return 0
-            return W - max(qt, 1) * P
+            return W if n > 0 else qt * P
 
         def main_max(i):
-            h, n, qt = tiles[i]
-            m_main = stat.tile([P, 1], F32, name="m_main")
-            nc.vector.tensor_reduce(out=m_main[:], in_=s_main[i % 3][:, lo_col(i):W], axis=AX.X, op=ALU.max)
-            state[("mm", i)] = m_main
+            if has_main(i):
+                m_main = stat.tile([P, 1], F32, name="m_main")
+                nc.vector.tensor_reduce(out=m_main[:], in_=s_main[i % 3][:, 0:live(i)], axis=AX.X, op=ALU.max)
+                state[("mm", i)] = m_main
 
         def combine(i):
             h, n, qt = tiles[i]
-            m_main = state[("mm", i)]
+            me = bstate[("me", i // SUBS)][:, qt:qt + 1]
+            m_main = state[("mm", i)][:] if has_main(i) else me
             nm = stat.tile([P, 1], F32, name="nm")
-            nc.vector.tensor_scalar(out=nm[:], in0=m_main[:], scalar1=bstate[("me", i // SUBS)][:, qt:qt + 1],
-                                    scalar2=-SCALE, op0=ALU.max, op1=ALU.mult)
+            nc.vector.tensor_scalar(out=nm[:], in0=m_main, scalar1=me, scalar2=-SCALE, op0=ALU.max, op1=ALU.mult)
             state[("nm", i)] = nm
 
         def exps(i):
@@ -209,61 +233,81 @@ def tile_baseattention_t_kernel(tc, q, k, v, out):
             b = i // SUBS
             nm = state[("nm", i)]
             dn = bstate[("dn", b)]
-            e_sb = e_bufs[i % (2 * SUBS)]
-            lo = lo_col(i)
-            c0 = qt * P
-            nc.scalar.activation(out=e_sb[:, c0 + lo:c0 + W], in_=s_main[i % 3][:, lo:W], func=ACTF.Exp,
-                                 bias=nm[:], scale=SCALE, accum_out=dn[:, 0, qt:qt + 1])
-            nc.scalar.activation(out=e_sb[:, c0 + W:c0 + W + P], in_=s_edge[b % 2][:, qt, :], func=ACTF.Exp,
-                                 bias=nm[:], scale=SCALE, accum_out=dn[:, 1, qt:qt + 1])
-            state[("e", i)] = e_sb
+            if has_main(i):
+                e_sb = ep.tile([P, 2, P, 2], BF16, name="e_sb")
+                lv = live(i)
+                if lv < W:
+                    nc.gpsimd.memset(e_sb[:, :, lv // 4:, :], 0.0)
+                nc.scalar.activation(out=e_sb[:, :, 0:lv // 4, :],
+                                     in_=s_main[i % 3][:, 0:lv].rearrange("p (w u e) -> p u w e", u=2, e=2),
+                                     func=ACTF.Exp, bias=nm[:], scale=SCALE, accum_out=dn[:, 0, qt:qt + 1])
+                state[("e", i)] = e_sb
+            e_diag = bstate[("ed", b)]
+            nc.scalar.activation(out=e_diag[:, :, qt, :, :],
+                                 in_=s_edge[b % 2][:, qt, :].rearrange("p (w u e) -> p u w e", u=2, e=2),
+                                 func=ACTF.Exp, bias=nm[:], scale=SCALE, accum_out=dn[:, 1, qt:qt + 1])
 
         def flip_pe(i):
             h, n, qt = tiles[i]
-            e_sb = state[("e", i)]
-            t_ps = next_flip()
-            for a in range(0 if n > 0 else 1, 2):
-                for t in range(4):
-                    nc.tensor.transpose(t_ps[:, 4 * a + t, :], e_sb[:, a * W + t:(a + 1) * W:4], ident[:])
-            state[("t", i)] = t_ps
+            b = i // SUBS
+            t_ps = flipped[i % 2]
+            if has_main(i):
+                words = state[("e", i)][:].rearrange("p u w e -> p (u w e)").bitcast(F32)
+                for u in range(2):
+                    nc.tensor.transpose(t_ps[:, u, :], words[:, u * P:(u + 1) * P], ident_f[:])
+            if qt == SUBS - 1:
+                words = bstate[("ed", b)][:].rearrange("p u j w e -> p (u j w e)").bitcast(F32)
+                for u in range(2):
+                    nc.tensor.transpose(t_ps[:, 2 + u, :], words[:, u * P:(u + 1) * P], ident_f[:])
 
         def regroup(i):
             h, n, qt = tiles[i]
-            t_ps = state[("t", i)]
-            g = grouped[qt]
-            ra = SUBS - qt
-            passes = [(qt + 1, 1)]
-            if n > 0:
-                passes.append((ra, 0))
-            for r, a in sorted(passes):
-                if r <= SMALL:
-                    t_sb = tsp.tile([P, 4, P], BF16, name="t_sb")
-                    nc.scalar.copy(out=t_sb[:], in_=t_ps[:, 4 * a:4 * a + 4, :])
-                    nc.gpsimd.tensor_scalar(out=g[:, a, :, :], in0=t_sb[:].rearrange("p t c -> p c t"),
-                                            scalar1=1.0, scalar2=0.0, op0=ALU.mult, op1=ALU.add)
-                else:
-                    nc.scalar.copy(out=g[:, a, :, :], in_=t_ps[:, 4 * a:4 * a + 4, :].rearrange("p t c -> p c t"))
+            b = i // SUBS
+            t_ps = flipped[i % 2]
+            if qt == 0:
+                bstate[("g", b)] = gp.tile([P, SUBS + 1, P, 4], BF16, name="grouped", align_bytes=64)
+            gw = bstate[("g", b)][:].rearrange("p x r t -> p (x r t)").bitcast(F32).rearrange("p (x r u) -> p x r u", r=P, u=2)
+            if qt == SUBS - 1:
+                nc.scalar.copy(out=gw[:, qt:qt + 2, :, :], in_=t_ps[:].rearrange("p (x u) r -> p x r u", u=2))
+            elif has_main(i):
+                nc.scalar.copy(out=gw[:, qt, :, :], in_=t_ps[:, 0:2, :].rearrange("p u r -> p r u"))
 
         def quant(i):
             h, n, qt = tiles[i]
-            g = grouped[qt]
-            e_words = wp.tile([P, 2 * P], U32, name="e_words", align_bytes=64)
-            e_scales = wp.tile([P, 2 * P], U8, name="e_scales", align_bytes=64)
-            a0 = 0 if n > 0 else 1
-            nc.vector.quantize_mx(out=e_words[:, a0 * P:].bitcast(FP8X4), scales=e_scales[:, a0 * P:],
-                                  in_=g[:, a0:, :, :].rearrange("p a c t -> p (a c t)"))
-            state[("w", i)] = (e_words, e_scales)
+            b = i // SUBS
+            if qt == 0:
+                bstate[("w", b)] = (wp.tile([P, SUBS + 1, P], I32, name="e_words", align_bytes=64),
+                                    wp.tile([P, SUBS + 1, P], U8, name="e_scales", align_bytes=64))
+            e_words, e_scales = bstate[("w", b)]
+            g = bstate[("g", b)]
+            todo = []
+            if has_main(i):
+                todo.append(qt)
+            if qt == SUBS - 1:
+                todo.append(SUBS)
+            for x in todo:
+                nc.vector.quantize_mx(out=e_words[:, x, :].bitcast(FP8X4), scales=e_scales[:, x, :],
+                                      in_=g[:, x, :, :].rearrange("p r t -> p (r t)"))
 
-        def mx(i):
-            h, n, qt = tiles[i]
-            e_words, e_scales = state[("w", i)]
-            a0 = 0 if n > 0 else 1
-            for a in range(a0, 2):
-                nc.tensor.matmul_mx(out=o_ps[:, qt, :], lhsT=e_words[:, a * P:(a + 1) * P].bitcast(FP8X4),
-                                    lhsT_scale=e_scales[:, a * P:(a + 1) * P],
-                                    rhs=v_words[h][:, n - 1 + a, :].bitcast(FP8X4),
-                                    rhs_scale=v_scales[h][:, n - 1 + a, :],
-                                    start=(a == a0), stop=(a == 1))
+        def mx(b):
+            h, n = blocks[b]
+            e_words, e_scales = bstate[("w", b)]
+            own = v_own[b % NVQ]
+            prev = v_own[(b - 1) % NVQ]
+            for qt in range(SUBS):
+                ops = []
+                if has_main(b * SUBS + qt):
+                    if n == 0:
+                        ops.append((qt, own[:]))
+                    elif qt == 0:
+                        ops.append((qt, prev[:]))
+                    else:
+                        ops.append((qt, v_mix[b % NVM][:, qt - 1, :]))
+                ops.append((SUBS, v_diag[b % NVM][:, qt, :]))
+                for x, vop in ops:
+                    nc.tensor.matmul_mx(out=o_ps[:, qt, :], lhsT=e_words[:, x, :].bitcast(FP8X4),
+                                        lhsT_scale=e_scales[:, x, :], rhs=codes(vop), rhs_scale=scales(vop),
+                                        start=(x == ops[0][0]), stop=(x == SUBS))
 
         def den_add(b):
             dn = bstate[("dn", b)]
@@ -286,36 +330,40 @@ def tile_baseattention_t_kernel(tc, q, k, v, out):
             nc.sync.dma_start(out=ov[:, r0:r0 + SUBS, :], in_=o_sb[:])
 
         for b in range(2):
-            prep_pe(b, flipped[b][:])
+            prep_pe(b, flip_bf[b])
             prep_copy(b)
             prep_v(b)
         quant_v(0)
+        spread_v(0)
         quant_v(1)
+        spread_v(1)
         edge_pe(0)
         edge_max(0)
 
         def ok(i):
             return 0 <= i < NT
 
-        for s in range(NT + L_OUT + SUBS):
+        def block_end(i):
+            return ok(i) and i % SUBS == SUBS - 1
+
+        for s in range(NT + L_OUT):
             ph = s % SUBS
-            i_out = s - L_OUT
-            if i_out >= SUBS - 1 and i_out % SUBS == SUBS - 1 and i_out < NT:
-                finish(i_out // SUBS)
+            if block_end(s - L_OUT):
+                finish((s - L_OUT) // SUBS)
             if s % (NB * SUBS) in (4, 12) and s // (NB * SUBS) + 1 < H:
-                half = 0 if s % (NB * SUBS) == 4 else NS // 2
-                load(s // (NB * SUBS) + 1, half, half + NS // 2)
+                half = 0 if s % (NB * SUBS) == 4 else NB // 2
+                load(s // (NB * SUBS) + 1, half, half + NB // 2)
             if ok(s - L_FLIP):
                 flip_pe(s - L_FLIP)
             b_prep = s // SUBS + 2
             if ph == 2 and b_prep < NBLK:
                 prep_pe(b_prep, edge_bf[(s // SUBS + 1) % 2])
             if ok(s):
-                main_pe_first(s)
-            if ok(s - L_MX):
-                mx(s - L_MX)
+                main_pe_prev(s)
+            if block_end(s - L_MX):
+                mx((s - L_MX) // SUBS)
             if ok(s):
-                main_pe_rest(s)
+                main_pe_own(s)
             b_edge = s // SUBS + 1
             if ph == 3 and b_edge < NBLK:
                 edge_pe(b_edge)
@@ -330,7 +378,7 @@ def tile_baseattention_t_kernel(tc, q, k, v, out):
             if ok(s - L_FLIP):
                 regroup(s - L_FLIP)
             i_den = s - L_EXP - 1
-            den_due = i_den >= 0 and i_den % SUBS == SUBS - 1 and i_den < NT
+            den_due = block_end(i_den)
             if den_due:
                 den_add(i_den // SUBS)
             if ph == 0 and 0 < s // SUBS < NBLK:
@@ -341,5 +389,6 @@ def tile_baseattention_t_kernel(tc, q, k, v, out):
                 prep_v(b_prep)
             if ph == 1 and 1 < s // SUBS + 1 < NBLK:
                 quant_v(s // SUBS + 1)
+                spread_v(s // SUBS + 1)
             if den_due:
                 den_recip(i_den // SUBS)

@@ -348,22 +348,19 @@ def tile_baseattention_t_kernel(tc, q, k, v, out):
 
         for s in range(NT + L_OUT):
             ph = s % SUBS
-            if block_end(s - L_OUT):
-                finish((s - L_OUT) // SUBS)
             if s % (NB * SUBS) in (4, 12) and s // (NB * SUBS) + 1 < H:
                 half = 0 if s % (NB * SUBS) == 4 else NB // 2
                 load(s // (NB * SUBS) + 1, half, half + NB // 2)
+            if ok(s):
+                main_pe_prev(s)
+                main_pe_own(s)
             if ok(s - L_FLIP):
                 flip_pe(s - L_FLIP)
             b_prep = s // SUBS + 2
             if ph == 2 and b_prep < NBLK:
                 prep_pe(b_prep, edge_bf[(s // SUBS + 1) % 2])
-            if ok(s):
-                main_pe_prev(s)
             if block_end(s - L_MX):
                 mx((s - L_MX) // SUBS)
-            if ok(s):
-                main_pe_own(s)
             b_edge = s // SUBS + 1
             if ph == 3 and b_edge < NBLK:
                 edge_pe(b_edge)
@@ -373,6 +370,8 @@ def tile_baseattention_t_kernel(tc, q, k, v, out):
                 quant(s - L_QUANT)
             if ok(s - L_MAX):
                 combine(s - L_MAX)
+            if block_end(s - L_OUT):
+                finish((s - L_OUT) // SUBS)
             if ok(s - L_EXP):
                 exps(s - L_EXP)
             if ok(s - L_FLIP):
@@ -390,5 +389,5 @@ def tile_baseattention_t_kernel(tc, q, k, v, out):
             if ph == 1 and 1 < s // SUBS + 1 < NBLK:
                 quant_v(s // SUBS + 1)
                 spread_v(s // SUBS + 1)
-            if den_due:
-                den_recip(i_den // SUBS)
+            if block_end(i_den - 1):
+                den_recip((i_den - 1) // SUBS)

@@ -28,9 +28,10 @@ VW = P + P // 4
 L_MAX = 1
 L_EXP = 2
 L_FLIP = 3
-L_QUANT = 4
+L_QUANT = 5
 L_MX = 6
 L_OUT = 7
+QT_VECTOR = 0
 
 
 def tile_baseattention_t_kernel(tc, q, k, v, out):
@@ -66,7 +67,8 @@ def tile_baseattention_t_kernel(tc, q, k, v, out):
             nc.sync.dma_start(out=k_raw[h][:, a:b, :], in_=kv[:, h * NS + a:h * NS + b, :])
             nc.sync.dma_start(out=v_raw[h][:, n0:n1, :, :], in_=vv[:, h * NB + n0:h * NB + n1, :, :])
 
-        load(0, 0, 2)
+        load(0, 0, 1)
+        load(0, 1, 2)
         load(0, 2, 4)
         load(0, 4, NB)
 
@@ -94,22 +96,22 @@ def tile_baseattention_t_kernel(tc, q, k, v, out):
         v_diag = []
         for j in range(NVQ):
             t = const.tile([P, VW], I32, name="v_own%d" % j, align_bytes=64)
-            nc.gpsimd.memset(t[:], 0)
+            nc.vector.memset(t[:], 0)
             v_own.append(t)
         for j in range(NVM):
             t = const.tile([P, SUBS - 1, VW], I32, name="v_mix%d" % j, align_bytes=64)
             v_mix.append(t)
             u = const.tile([P, SUBS, VW], I32, name="v_diag%d" % j, align_bytes=64)
-            nc.gpsimd.memset(u[:], 0)
+            nc.vector.memset(u[:], 0)
             v_diag.append(u)
 
         s_main = [psum.tile([P, W], F32, name="s_main%d" % j) for j in range(3)]
         s_edge = [psum.tile([P, SUBS, P], F32, name="s_edge%d" % j) for j in range(2)]
         flipped = [psum.tile([P, 4, P], F32, name="flipped%d" % j) for j in range(2)]
         o_ps = psum.tile([P, SUBS, P], F32, name="o_ps")
-        edge_bf = [t[:].rearrange("p j c -> p (j c)").bitcast(BF16).rearrange("p (j c) -> p j c", c=P) for t in s_edge]
         flip_bf = [t[:].rearrange("p j c -> p (j c)").bitcast(BF16).rearrange("p (j c) -> p j c", c=P) for t in flipped]
 
+        o_bf = o_ps[:].rearrange("p j c -> p (j c)").bitcast(BF16).rearrange("p (j c) -> p j c", c=P)
         tiles = [(h, n, qt) for h in range(H) for n in range(NB) for qt in range(SUBS)]
         blocks = [(h, n) for h in range(H) for n in range(NB)]
         NT = len(tiles)
@@ -132,7 +134,9 @@ def tile_baseattention_t_kernel(tc, q, k, v, out):
         def prep_copy(b):
             h, n = blocks[b]
             p_ps = bstate[("p", b)]
-            nc.scalar.copy(out=xT[h][:, :, n * W:(n + 1) * W], in_=p_ps.rearrange("p (a j) c -> p a (j c)", a=2))
+            dst = xT[h][:, :, n * W:(n + 1) * W]
+            src = p_ps.rearrange("p (a j) c -> p a (j c)", a=2)
+            nc.scalar.copy(out=dst, in_=src)
 
         def prep_v(b):
             h, n = blocks[b]
@@ -267,7 +271,9 @@ def tile_baseattention_t_kernel(tc, q, k, v, out):
             if qt == 0:
                 bstate[("g", b)] = gp.tile([P, SUBS + 1, P, 4], BF16, name="grouped", align_bytes=64)
             gw = bstate[("g", b)][:].rearrange("p x r t -> p (x r t)").bitcast(F32).rearrange("p (x r u) -> p x r u", r=P, u=2)
-            if qt == SUBS - 1:
+            if qt == QT_VECTOR and has_main(i):
+                nc.vector.tensor_copy(out=gw[:, qt, :, :], in_=t_ps[:, 0:2, :].rearrange("p u r -> p r u"))
+            elif qt == SUBS - 1:
                 nc.scalar.copy(out=gw[:, qt:qt + 2, :, :], in_=t_ps[:].rearrange("p (x u) r -> p x r u", u=2))
             elif has_main(i):
                 nc.scalar.copy(out=gw[:, qt, :, :], in_=t_ps[:, 0:2, :].rearrange("p u r -> p r u"))
@@ -329,16 +335,14 @@ def tile_baseattention_t_kernel(tc, q, k, v, out):
             r0 = h * NS + n * SUBS
             nc.sync.dma_start(out=ov[:, r0:r0 + SUBS, :], in_=o_sb[:])
 
-        for b in range(2):
-            prep_pe(b, flip_bf[b])
-            prep_copy(b)
-            prep_v(b)
-        quant_v(0)
-        spread_v(0)
-        quant_v(1)
-        spread_v(1)
+        prep_pe(0, flip_bf[0])
+        prep_copy(0)
         edge_pe(0)
+        prep_v(0)
         edge_max(0)
+        prep_pe(1, o_bf)
+        prep_copy(1)
+        prep_v(1)
 
         def ok(i):
             return 0 <= i < NT
@@ -348,22 +352,23 @@ def tile_baseattention_t_kernel(tc, q, k, v, out):
 
         for s in range(NT + L_OUT):
             ph = s % SUBS
+            blk = s // SUBS
             if s % (NB * SUBS) in (4, 12) and s // (NB * SUBS) + 1 < H:
                 half = 0 if s % (NB * SUBS) == 4 else NB // 2
                 load(s // (NB * SUBS) + 1, half, half + NB // 2)
+            if ok(s - L_FLIP):
+                flip_pe(s - L_FLIP)
             if ok(s):
                 main_pe_prev(s)
                 main_pe_own(s)
-            if ok(s - L_FLIP):
-                flip_pe(s - L_FLIP)
-            b_prep = s // SUBS + 2
-            if ph == 2 and b_prep < NBLK:
-                prep_pe(b_prep, edge_bf[(s // SUBS + 1) % 2])
+            if ph == 3 and blk + 2 < NBLK:
+                prep_pe(blk + 2, o_bf)
             if block_end(s - L_MX):
                 mx((s - L_MX) // SUBS)
-            b_edge = s // SUBS + 1
-            if ph == 3 and b_edge < NBLK:
-                edge_pe(b_edge)
+            if ph == 3 and blk + 1 < NBLK:
+                edge_pe(blk + 1)
+            if ph == 1 and 0 < blk < NBLK:
+                edge_max(blk)
             if ok(s - L_MAX):
                 main_max(s - L_MAX)
             if ok(s - L_QUANT):
@@ -377,17 +382,17 @@ def tile_baseattention_t_kernel(tc, q, k, v, out):
             if ok(s - L_FLIP):
                 regroup(s - L_FLIP)
             i_den = s - L_EXP - 1
-            den_due = block_end(i_den)
-            if den_due:
+            if block_end(i_den):
                 den_add(i_den // SUBS)
-            if ph == 0 and 0 < s // SUBS < NBLK:
-                edge_max(s // SUBS)
-            if ph == 2 and b_prep < NBLK:
-                prep_copy(b_prep)
-            if ph == 3 and b_prep < NBLK:
-                prep_v(b_prep)
-            if ph == 1 and 1 < s // SUBS + 1 < NBLK:
-                quant_v(s // SUBS + 1)
-                spread_v(s // SUBS + 1)
+            if ph == 0 and 0 < blk and blk + 1 < NBLK:
+                prep_copy(blk + 1)
+            if ph == 3 and blk + 2 < NBLK:
+                prep_v(blk + 2)
+            if s == 0:
+                quant_v(0)
+                spread_v(0)
+            if ph == 1 and blk + 1 < NBLK:
+                quant_v(blk + 1)
+                spread_v(blk + 1)
             if block_end(i_den - 1):
                 den_recip((i_den - 1) // SUBS)

@@ -24,13 +24,26 @@ SCALE = 128.0 ** -0.5
 NEG = -(2.0 ** 80)
 FLOPS = 2 * (2 * NB - 1) * H * 2 * W * W * P
 VW = P + P // 4
+NVQ = 7
+NVM = 5
 
-L_MAX = 1
-L_EXP = 2
-L_FLIP = 3
-L_QUANT = 5
-L_MX = 6
-L_OUT = 7
+AT_MAX = 1
+AT_EXP = 2
+AT_FLIP = 4
+AT_COPY = 4
+AT_QUANT = 6
+AT_PREP = -4
+AT_PREP_COPY = -3
+AT_EDGE = 0
+AT_EDGE_MAX = 1
+AT_EDGE_FLIP = 6
+AT_SUM = 6
+AT_RECIP = 8
+AT_EDGE_QUANT = 8
+AT_MX = 10
+AT_OUT = 11
+AT_V_GROUP = -5
+AT_V_QUANT = -3
 QT_VECTOR = 0
 
 
@@ -44,11 +57,11 @@ def tile_baseattention_t_kernel(tc, q, k, v, out):
     with ExitStack() as ctx:
         const = ctx.enter_context(tc.tile_pool(name="const", bufs=1))
         stat = ctx.enter_context(tc.tile_pool(name="stat", bufs=4))
-        ep = ctx.enter_context(tc.tile_pool(name="ep", bufs=3))
+        ep = ctx.enter_context(tc.tile_pool(name="ep", bufs=4))
         gp = ctx.enter_context(tc.tile_pool(name="gp", bufs=3))
         wp = ctx.enter_context(tc.tile_pool(name="wp", bufs=3))
         vgp = ctx.enter_context(tc.tile_pool(name="vgp", bufs=2))
-        op = ctx.enter_context(tc.tile_pool(name="op", bufs=3))
+        op = ctx.enter_context(tc.tile_pool(name="op", bufs=2))
         psum = ctx.enter_context(tc.psum_pool(name="psum", bufs=1))
         ctx.enter_context(tc.manual_schedule())
 
@@ -89,8 +102,6 @@ def tile_baseattention_t_kernel(tc, q, k, v, out):
         xT = []
         for h in range(H):
             xT.append(const.tile([P, 2, T], BF16, name="xT%d" % h))
-        NVQ = 6
-        NVM = 4
         v_own = []
         v_mix = []
         v_diag = []
@@ -100,6 +111,7 @@ def tile_baseattention_t_kernel(tc, q, k, v, out):
             v_own.append(t)
         for j in range(NVM):
             t = const.tile([P, SUBS - 1, VW], I32, name="v_mix%d" % j, align_bytes=64)
+            nc.vector.memset(t[:], 0)
             v_mix.append(t)
             u = const.tile([P, SUBS, VW], I32, name="v_diag%d" % j, align_bytes=64)
             nc.vector.memset(u[:], 0)
@@ -109,9 +121,9 @@ def tile_baseattention_t_kernel(tc, q, k, v, out):
         s_edge = [psum.tile([P, SUBS, P], F32, name="s_edge%d" % j) for j in range(2)]
         flipped = [psum.tile([P, 4, P], F32, name="flipped%d" % j) for j in range(2)]
         o_ps = psum.tile([P, SUBS, P], F32, name="o_ps")
-        flip_bf = [t[:].rearrange("p j c -> p (j c)").bitcast(BF16).rearrange("p (j c) -> p j c", c=P) for t in flipped]
-
         o_bf = o_ps[:].rearrange("p j c -> p (j c)").bitcast(BF16).rearrange("p (j c) -> p j c", c=P)
+        flip_bf = flipped[0][:].rearrange("p j c -> p (j c)").bitcast(BF16).rearrange("p (j c) -> p j c", c=P)
+
         tiles = [(h, n, qt) for h in range(H) for n in range(NB) for qt in range(SUBS)]
         blocks = [(h, n) for h in range(H) for n in range(NB)]
         NT = len(tiles)
@@ -123,22 +135,22 @@ def tile_baseattention_t_kernel(tc, q, k, v, out):
             h, n, qt = tiles[i]
             return n > 0 or qt > 0
 
+        def lo_col(i):
+            h, n, qt = tiles[i]
+            return 0 if n > 0 else W - qt * P
+
         def prep_pe(b, p_ps):
             h, n = blocks[b]
             for j in range(SUBS):
                 nc.tensor.transpose(p_ps[:, j, :], q_raw[h][:, n * SUBS + j, :], ident[:])
             for j in range(SUBS):
                 nc.tensor.transpose(p_ps[:, SUBS + j, :], k_raw[h][:, n * SUBS + j, :], ident[:])
-            bstate[("p", b)] = p_ps
 
-        def prep_copy(b):
+        def prep_copy(b, p_ps):
             h, n = blocks[b]
-            p_ps = bstate[("p", b)]
-            dst = xT[h][:, :, n * W:(n + 1) * W]
-            src = p_ps.rearrange("p (a j) c -> p a (j c)", a=2)
-            nc.scalar.copy(out=dst, in_=src)
+            nc.scalar.copy(out=xT[h][:, :, n * W:(n + 1) * W], in_=p_ps.rearrange("p (a j) c -> p a (j c)", a=2))
 
-        def prep_v(b):
+        def group_v(b):
             h, n = blocks[b]
             v_g = vgp.tile([P, P, 4], BF16, name="v_g", align_bytes=64)
             nc.gpsimd.tensor_scalar(out=v_g[:], in0=v_raw[h][:, n, :, :].rearrange("p t d -> p d t"),
@@ -152,10 +164,9 @@ def tile_baseattention_t_kernel(tc, q, k, v, out):
             return ap[:, P:VW].bitcast(U8)
 
         def quant_v(b):
-            h, n = blocks[b]
-            v_g = bstate[("vg", b)]
             own = v_own[b % NVQ]
-            nc.vector.quantize_mx(out=codes(own), scales=scales(own), in_=v_g[:].rearrange("p d t -> p (d t)"))
+            nc.vector.quantize_mx(out=codes(own), scales=scales(own),
+                                  in_=bstate[("vg", b)][:].rearrange("p d t -> p (d t)"))
 
         def spread_v(b):
             h, n = blocks[b]
@@ -166,12 +177,17 @@ def tile_baseattention_t_kernel(tc, q, k, v, out):
             for j in range(SUBS):
                 rows = slice(j * Q, (j + 1) * Q)
                 nc.sync.dma_start(out=diag[rows, j, :], in_=own[rows, :])
+            for qt in range(1, SUBS):
+                pieces = [(own, 0, SUBS - qt, qt)]
                 if n > 0:
-                    if j < SUBS - 1:
-                        r = SUBS - 1 - j
-                        nc.sync.dma_start(out=mix[rows, j:, :], in_=own[rows, :].unsqueeze(1).to_broadcast([Q, r, VW]))
-                    if j > 0:
-                        nc.sync.dma_start(out=mix[rows, 0:j, :], in_=prev[rows, :].unsqueeze(1).to_broadcast([Q, j, VW]))
+                    pieces.append((prev, qt, 0, SUBS - qt))
+                for src, s0, d0, cnt in pieces:
+                    while cnt > 0:
+                        m = min(cnt, 2)
+                        nc.sync.dma_start(out=mix[d0 * Q:(d0 + m) * Q, qt - 1, :], in_=src[s0 * Q:(s0 + m) * Q, :])
+                        s0 += m
+                        d0 += m
+                        cnt -= m
 
         def edge_pe(b):
             h, n = blocks[b]
@@ -189,39 +205,27 @@ def tile_baseattention_t_kernel(tc, q, k, v, out):
             dn = stat.tile([P, 2, SUBS], F32, name="dn")
             if blocks[b][1] == 0:
                 nc.gpsimd.memset(dn[:, 0, 0:1], 0.0)
+            e_diag = ep.tile([P, 2, SUBS, Q, 2], BF16, name="e_diag")
             bstate[("me", b)] = m_edge
             bstate[("dn", b)] = dn
-            e_diag = ep.tile([P, 2, SUBS, Q, 2], BF16, name="e_diag")
             bstate[("ed", b)] = e_diag
 
-        def main_pe_prev(i):
+        def main_pe(i):
             h, n, qt = tiles[i]
-            if n == 0:
+            if not has_main(i):
                 return
             sm = s_main[i % 3]
             row = n * SUBS + qt
-            qT = xT[h][:, 0, row * P:(row + 1) * P]
-            k0 = (row - SUBS) * P
-            nc.tensor.matmul(sm[:, qt * P:W], lhsT=qT, rhs=xT[h][:, 1, k0:n * W], start=True, stop=False)
-            nc.tensor.matmul(sm[:, qt * P:(qt + 1) * P], lhsT=ident[:], rhs=mask[:, 0, :], start=False, stop=True)
-
-        def main_pe_own(i):
-            h, n, qt = tiles[i]
-            if qt == 0:
-                return
-            sm = s_main[i % 3]
-            row = n * SUBS + qt
-            qT = xT[h][:, 0, row * P:(row + 1) * P]
-            nc.tensor.matmul(sm[:, 0:qt * P], lhsT=qT, rhs=xT[h][:, 1, n * W:row * P], start=True, stop=True)
-
-        def live(i):
-            h, n, qt = tiles[i]
-            return W if n > 0 else qt * P
+            lo = lo_col(i)
+            nc.tensor.matmul(sm[:, lo:W], lhsT=xT[h][:, 0, row * P:(row + 1) * P],
+                             rhs=xT[h][:, 1, row * P - W + lo:row * P], start=True, stop=(n == 0))
+            if n > 0:
+                nc.tensor.matmul(sm[:, 0:P], lhsT=ident[:], rhs=mask[:, 0, :], start=False, stop=True)
 
         def main_max(i):
             if has_main(i):
                 m_main = stat.tile([P, 1], F32, name="m_main")
-                nc.vector.tensor_reduce(out=m_main[:], in_=s_main[i % 3][:, 0:live(i)], axis=AX.X, op=ALU.max)
+                nc.vector.tensor_reduce(out=m_main[:], in_=s_main[i % 3][:, lo_col(i):W], axis=AX.X, op=ALU.max)
                 state[("mm", i)] = m_main
 
         def combine(i):
@@ -239,89 +243,77 @@ def tile_baseattention_t_kernel(tc, q, k, v, out):
             dn = bstate[("dn", b)]
             if has_main(i):
                 e_sb = ep.tile([P, 2, P, 2], BF16, name="e_sb")
-                lv = live(i)
-                if lv < W:
-                    nc.gpsimd.memset(e_sb[:, :, lv // 4:, :], 0.0)
-                nc.scalar.activation(out=e_sb[:, :, 0:lv // 4, :],
-                                     in_=s_main[i % 3][:, 0:lv].rearrange("p (w u e) -> p u w e", u=2, e=2),
+                lo = lo_col(i)
+                if lo > 0:
+                    nc.gpsimd.memset(e_sb[:, :, 0:lo // 4, :], 0.0)
+                nc.scalar.activation(out=e_sb[:, :, lo // 4:, :],
+                                     in_=s_main[i % 3][:, lo:W].rearrange("p (w u e) -> p u w e", u=2, e=2),
                                      func=ACTF.Exp, bias=nm[:], scale=SCALE, accum_out=dn[:, 0, qt:qt + 1])
                 state[("e", i)] = e_sb
-            e_diag = bstate[("ed", b)]
-            nc.scalar.activation(out=e_diag[:, :, qt, :, :],
+            nc.scalar.activation(out=bstate[("ed", b)][:, :, qt, :, :],
                                  in_=s_edge[b % 2][:, qt, :].rearrange("p (w u e) -> p u w e", u=2, e=2),
                                  func=ACTF.Exp, bias=nm[:], scale=SCALE, accum_out=dn[:, 1, qt:qt + 1])
 
         def flip_pe(i):
-            h, n, qt = tiles[i]
-            b = i // SUBS
-            t_ps = flipped[i % 2]
             if has_main(i):
                 words = state[("e", i)][:].rearrange("p u w e -> p (u w e)").bitcast(F32)
                 for u in range(2):
-                    nc.tensor.transpose(t_ps[:, u, :], words[:, u * P:(u + 1) * P], ident_f[:])
-            if qt == SUBS - 1:
-                words = bstate[("ed", b)][:].rearrange("p u j w e -> p (u j w e)").bitcast(F32)
-                for u in range(2):
-                    nc.tensor.transpose(t_ps[:, 2 + u, :], words[:, u * P:(u + 1) * P], ident_f[:])
+                    nc.tensor.transpose(flipped[i // 2 % 2][:, 2 * (i % 2) + u, :], words[:, u * P:(u + 1) * P],
+                                        ident_f[:])
+
+        def edge_flip(b):
+            words = bstate[("ed", b)][:].rearrange("p u j w e -> p (u j w e)").bitcast(F32)
+            for u in range(2):
+                nc.tensor.transpose(s_edge[b % 2][:, u, :], words[:, u * P:(u + 1) * P], ident_f[:])
+
+        def grouped_words(b):
+            if ("g", b) not in bstate:
+                bstate[("g", b)] = gp.tile([P, SUBS + 1, P, 4], BF16, name="grouped", align_bytes=64)
+            g = bstate[("g", b)]
+            return g[:].rearrange("p x r t -> p (x r t)").bitcast(F32).rearrange("p (x r u) -> p x r u", r=P, u=2)
 
         def regroup(i):
             h, n, qt = tiles[i]
-            b = i // SUBS
-            t_ps = flipped[i % 2]
-            if qt == 0:
-                bstate[("g", b)] = gp.tile([P, SUBS + 1, P, 4], BF16, name="grouped", align_bytes=64)
-            gw = bstate[("g", b)][:].rearrange("p x r t -> p (x r t)").bitcast(F32).rearrange("p (x r u) -> p x r u", r=P, u=2)
-            if qt == QT_VECTOR and has_main(i):
-                nc.vector.tensor_copy(out=gw[:, qt, :, :], in_=t_ps[:, 0:2, :].rearrange("p u r -> p r u"))
-            elif qt == SUBS - 1:
-                nc.scalar.copy(out=gw[:, qt:qt + 2, :, :], in_=t_ps[:].rearrange("p (x u) r -> p x r u", u=2))
-            elif has_main(i):
-                nc.scalar.copy(out=gw[:, qt, :, :], in_=t_ps[:, 0:2, :].rearrange("p u r -> p r u"))
+            if has_main(i):
+                r0 = 2 * (i % 2)
+                src = flipped[i // 2 % 2][:, r0:r0 + 2, :].rearrange("p u r -> p r u")
+                dst = grouped_words(i // SUBS)[:, qt, :, :]
+                if qt == QT_VECTOR:
+                    nc.vector.tensor_copy(out=dst, in_=src)
+                else:
+                    nc.scalar.copy(out=dst, in_=src)
 
-        def quant(i):
-            h, n, qt = tiles[i]
-            b = i // SUBS
-            if qt == 0:
+        def edge_regroup(b):
+            nc.scalar.copy(out=grouped_words(b)[:, SUBS, :, :], in_=s_edge[b % 2][:, 0:2, :].rearrange("p u r -> p r u"))
+
+        def quant(b, x):
+            if ("w", b) not in bstate:
                 bstate[("w", b)] = (wp.tile([P, SUBS + 1, P], I32, name="e_words", align_bytes=64),
                                     wp.tile([P, SUBS + 1, P], U8, name="e_scales", align_bytes=64))
             e_words, e_scales = bstate[("w", b)]
-            g = bstate[("g", b)]
-            todo = []
-            if has_main(i):
-                todo.append(qt)
-            if qt == SUBS - 1:
-                todo.append(SUBS)
-            for x in todo:
-                nc.vector.quantize_mx(out=e_words[:, x, :].bitcast(FP8X4), scales=e_scales[:, x, :],
-                                      in_=g[:, x, :, :].rearrange("p r t -> p (r t)"))
+            nc.vector.quantize_mx(out=e_words[:, x, :].bitcast(FP8X4), scales=e_scales[:, x, :],
+                                  in_=bstate[("g", b)][:, x, :, :].rearrange("p r t -> p (r t)"))
 
         def mx(b):
             h, n = blocks[b]
             e_words, e_scales = bstate[("w", b)]
-            own = v_own[b % NVQ]
-            prev = v_own[(b - 1) % NVQ]
             for qt in range(SUBS):
                 ops = []
                 if has_main(b * SUBS + qt):
-                    if n == 0:
-                        ops.append((qt, own[:]))
-                    elif qt == 0:
-                        ops.append((qt, prev[:]))
-                    else:
-                        ops.append((qt, v_mix[b % NVM][:, qt - 1, :]))
+                    ops.append((qt, v_own[(b - 1) % NVQ][:] if qt == 0 else v_mix[b % NVM][:, qt - 1, :]))
                 ops.append((SUBS, v_diag[b % NVM][:, qt, :]))
                 for x, vop in ops:
                     nc.tensor.matmul_mx(out=o_ps[:, qt, :], lhsT=e_words[:, x, :].bitcast(FP8X4),
                                         lhsT_scale=e_scales[:, x, :], rhs=codes(vop), rhs_scale=scales(vop),
                                         start=(x == ops[0][0]), stop=(x == SUBS))
 
-        def den_add(b):
+        def sum_up(b):
             dn = bstate[("dn", b)]
             ds = stat.tile([P, SUBS], F32, name="ds")
             nc.vector.tensor_tensor(out=ds[:], in0=dn[:, 0, :], in1=dn[:, 1, :], op=ALU.add)
             bstate[("ds", b)] = ds
 
-        def den_recip(b):
+        def recip(b):
             rd = stat.tile([P, SUBS], F32, name="rd")
             nc.vector.reciprocal(out=rd[:], in_=bstate[("ds", b)][:])
             bstate[("rd", b)] = rd
@@ -335,64 +327,56 @@ def tile_baseattention_t_kernel(tc, q, k, v, out):
             r0 = h * NS + n * SUBS
             nc.sync.dma_start(out=ov[:, r0:r0 + SUBS, :], in_=o_sb[:])
 
-        prep_pe(0, flip_bf[0])
-        prep_copy(0)
-        edge_pe(0)
-        prep_v(0)
-        edge_max(0)
+        prep_pe(0, flip_bf)
+        prep_copy(0, flip_bf)
+        group_v(0)
         prep_pe(1, o_bf)
-        prep_copy(1)
-        prep_v(1)
+        group_v(1)
 
-        def ok(i):
-            return 0 <= i < NT
+        def tile_at(s, at):
+            return s - at if 0 <= s - at < NT else None
 
-        def block_end(i):
-            return ok(i) and i % SUBS == SUBS - 1
+        def block_at(s, at, first=0):
+            b = (s - at) // SUBS
+            return b if (s - at) % SUBS == 0 and first <= b < NBLK else None
 
-        for s in range(NT + L_OUT):
-            ph = s % SUBS
-            blk = s // SUBS
+        def when(x, f, *args):
+            if x is not None:
+                f(x, *args)
+
+        def quant_tile(i):
+            if has_main(i):
+                quant(i // SUBS, i % SUBS)
+
+        def quant_and_spread_v(b):
+            quant_v(b)
+            spread_v(b)
+
+        for s in range(NT + AT_OUT):
             if s % (NB * SUBS) in (4, 12) and s // (NB * SUBS) + 1 < H:
                 half = 0 if s % (NB * SUBS) == 4 else NB // 2
                 load(s // (NB * SUBS) + 1, half, half + NB // 2)
-            if ok(s - L_FLIP):
-                flip_pe(s - L_FLIP)
-            if ok(s):
-                main_pe_prev(s)
-                main_pe_own(s)
-            if ph == 3 and blk + 2 < NBLK:
-                prep_pe(blk + 2, o_bf)
-            if block_end(s - L_MX):
-                mx((s - L_MX) // SUBS)
-            if ph == 3 and blk + 1 < NBLK:
-                edge_pe(blk + 1)
-            if ph == 1 and 0 < blk < NBLK:
-                edge_max(blk)
-            if ok(s - L_MAX):
-                main_max(s - L_MAX)
-            if ok(s - L_QUANT):
-                quant(s - L_QUANT)
-            if ok(s - L_MAX):
-                combine(s - L_MAX)
-            if block_end(s - L_OUT):
-                finish((s - L_OUT) // SUBS)
-            if ok(s - L_EXP):
-                exps(s - L_EXP)
-            if ok(s - L_FLIP):
-                regroup(s - L_FLIP)
-            i_den = s - L_EXP - 1
-            if block_end(i_den):
-                den_add(i_den // SUBS)
-            if ph == 0 and 0 < blk and blk + 1 < NBLK:
-                prep_copy(blk + 1)
-            if ph == 3 and blk + 2 < NBLK:
-                prep_v(blk + 2)
+            when(block_at(s, AT_EDGE), edge_pe)
+            if (s - AT_FLIP) % 2 == 0:
+                when(tile_at(s, AT_FLIP), flip_pe)
+                when(tile_at(s, AT_FLIP - 1), flip_pe)
+            when(block_at(s, AT_EDGE_FLIP), edge_flip)
+            when(block_at(s, AT_PREP, 2), prep_pe, o_bf)
+            when(tile_at(s, 0), main_pe)
+            when(block_at(s, AT_MX), mx)
+            when(block_at(s, AT_EDGE_MAX), edge_max)
+            when(tile_at(s, AT_MAX), main_max)
+            when(tile_at(s, AT_QUANT), quant_tile)
+            when(block_at(s, AT_EDGE_QUANT), quant, SUBS)
             if s == 0:
-                quant_v(0)
-                spread_v(0)
-            if ph == 1 and blk + 1 < NBLK:
-                quant_v(blk + 1)
-                spread_v(blk + 1)
-            if block_end(i_den - 1):
-                den_recip((i_den - 1) // SUBS)
+                quant_and_spread_v(0)
+            when(block_at(s, AT_V_QUANT, 1), quant_and_spread_v)
+            when(block_at(s, AT_OUT), finish)
+            when(block_at(s, AT_SUM), sum_up)
+            when(tile_at(s, AT_MAX), combine)
+            when(block_at(s, AT_RECIP), recip)
+            when(tile_at(s, AT_EXP), exps)
+            when(block_at(s, AT_PREP_COPY, 1), prep_copy, o_bf)
+            when(block_at(s, AT_EDGE_FLIP), edge_regroup)
+            when(tile_at(s, AT_COPY), regroup)
+            when(block_at(s, AT_V_GROUP, 2), group_v)

@@ -24,27 +24,27 @@ SCALE = 128.0 ** -0.5
 NEG = -(2.0 ** 80)
 FLOPS = 2 * (2 * NB - 1) * H * 2 * W * W * P
 VW = P + P // 4
-NVQ = 7
+NVQ = 6
 NVM = 5
 
 AT_MAX = 1
 AT_EXP = 2
 AT_FLIP = 4
 AT_COPY = 4
-AT_QUANT = 6
-AT_PREP = -4
-AT_PREP_COPY = -3
+AT_QUANT = 5
+AT_V_GROUP = -5
+AT_V_QUANT = -3
+AT_PREP = -3
 AT_EDGE = 0
 AT_EDGE_MAX = 1
 AT_EDGE_FLIP = 6
 AT_SUM = 6
-AT_RECIP = 8
-AT_EDGE_QUANT = 8
+AT_RECIP = 7
+AT_EDGE_QUANT = 9
 AT_MX = 10
 AT_OUT = 11
-AT_V_GROUP = -5
-AT_V_QUANT = -3
-QT_VECTOR = 0
+QT_VECTOR = 1
+ALONE = (0, 4, 5, 6)
 
 
 def tile_baseattention_t_kernel(tc, q, k, v, out):
@@ -61,7 +61,7 @@ def tile_baseattention_t_kernel(tc, q, k, v, out):
         gp = ctx.enter_context(tc.tile_pool(name="gp", bufs=3))
         wp = ctx.enter_context(tc.tile_pool(name="wp", bufs=3))
         vgp = ctx.enter_context(tc.tile_pool(name="vgp", bufs=2))
-        op = ctx.enter_context(tc.tile_pool(name="op", bufs=2))
+        op = ctx.enter_context(tc.tile_pool(name="op", bufs=4))
         psum = ctx.enter_context(tc.psum_pool(name="psum", bufs=1))
         ctx.enter_context(tc.manual_schedule())
 
@@ -103,19 +103,15 @@ def tile_baseattention_t_kernel(tc, q, k, v, out):
         for h in range(H):
             xT.append(const.tile([P, 2, T], BF16, name="xT%d" % h))
         v_own = []
-        v_mix = []
-        v_diag = []
+        v_spread = []
         for j in range(NVQ):
             t = const.tile([P, VW], I32, name="v_own%d" % j, align_bytes=64)
             nc.vector.memset(t[:], 0)
             v_own.append(t)
         for j in range(NVM):
-            t = const.tile([P, SUBS - 1, VW], I32, name="v_mix%d" % j, align_bytes=64)
+            t = const.tile([P, 7, VW], I32, name="v_spread%d" % j, align_bytes=64)
             nc.vector.memset(t[:], 0)
-            v_mix.append(t)
-            u = const.tile([P, SUBS, VW], I32, name="v_diag%d" % j, align_bytes=64)
-            nc.vector.memset(u[:], 0)
-            v_diag.append(u)
+            v_spread.append(t)
 
         s_main = [psum.tile([P, W], F32, name="s_main%d" % j) for j in range(3)]
         s_edge = [psum.tile([P, SUBS, P], F32, name="s_edge%d" % j) for j in range(2)]
@@ -135,9 +131,9 @@ def tile_baseattention_t_kernel(tc, q, k, v, out):
             h, n, qt = tiles[i]
             return n > 0 or qt > 0
 
-        def lo_col(i):
+        def hi_col(i):
             h, n, qt = tiles[i]
-            return 0 if n > 0 else W - qt * P
+            return W if n > 0 else qt * P
 
         def prep_pe(b, p_ps):
             h, n = blocks[b]
@@ -172,22 +168,19 @@ def tile_baseattention_t_kernel(tc, q, k, v, out):
             h, n = blocks[b]
             own = v_own[b % NVQ]
             prev = v_own[(b - 1) % NVQ]
-            mix = v_mix[b % NVM]
-            diag = v_diag[b % NVM]
-            for j in range(SUBS):
+
+            def put(src, j, slots, cnt):
                 rows = slice(j * Q, (j + 1) * Q)
-                nc.sync.dma_start(out=diag[rows, j, :], in_=own[rows, :])
-            for qt in range(1, SUBS):
-                pieces = [(own, 0, SUBS - qt, qt)]
-                if n > 0:
-                    pieces.append((prev, qt, 0, SUBS - qt))
-                for src, s0, d0, cnt in pieces:
-                    while cnt > 0:
-                        m = min(cnt, 2)
-                        nc.sync.dma_start(out=mix[d0 * Q:(d0 + m) * Q, qt - 1, :], in_=src[s0 * Q:(s0 + m) * Q, :])
-                        s0 += m
-                        d0 += m
-                        cnt -= m
+                nc.sync.dma_start(out=v_spread[b % NVM][rows, slots, :],
+                                  in_=src[rows, :].unsqueeze(1).to_broadcast([Q, cnt, VW]))
+
+            put(own, 0, slice(0, 4), 4)
+            put(own, 1, slice(2, 5), 3)
+            put(own, 2, slice(3, 6, 2), 2)
+            put(own, 3, slice(6, 7), 1)
+            if n > 0:
+                for j in range(1, SUBS):
+                    put(prev, j, slice(1, j + 1), j)
 
         def edge_pe(b):
             h, n = blocks[b]
@@ -212,20 +205,19 @@ def tile_baseattention_t_kernel(tc, q, k, v, out):
 
         def main_pe(i):
             h, n, qt = tiles[i]
-            if not has_main(i):
-                return
             sm = s_main[i % 3]
             row = n * SUBS + qt
-            lo = lo_col(i)
-            nc.tensor.matmul(sm[:, lo:W], lhsT=xT[h][:, 0, row * P:(row + 1) * P],
-                             rhs=xT[h][:, 1, row * P - W + lo:row * P], start=True, stop=(n == 0))
+            qT = xT[h][:, 0, row * P:(row + 1) * P]
             if n > 0:
-                nc.tensor.matmul(sm[:, 0:P], lhsT=ident[:], rhs=mask[:, 0, :], start=False, stop=True)
+                nc.tensor.matmul(sm[:, qt * P:W], lhsT=qT, rhs=xT[h][:, 1, row * P - W:n * W], start=True, stop=False)
+                nc.tensor.matmul(sm[:, qt * P:(qt + 1) * P], lhsT=ident[:], rhs=mask[:, 0, :], start=False, stop=True)
+            if qt > 0:
+                nc.tensor.matmul(sm[:, 0:qt * P], lhsT=qT, rhs=xT[h][:, 1, n * W:row * P], start=True, stop=True)
 
         def main_max(i):
             if has_main(i):
                 m_main = stat.tile([P, 1], F32, name="m_main")
-                nc.vector.tensor_reduce(out=m_main[:], in_=s_main[i % 3][:, lo_col(i):W], axis=AX.X, op=ALU.max)
+                nc.vector.tensor_reduce(out=m_main[:], in_=s_main[i % 3][:, 0:hi_col(i)], axis=AX.X, op=ALU.max)
                 state[("mm", i)] = m_main
 
         def combine(i):
@@ -243,11 +235,11 @@ def tile_baseattention_t_kernel(tc, q, k, v, out):
             dn = bstate[("dn", b)]
             if has_main(i):
                 e_sb = ep.tile([P, 2, P, 2], BF16, name="e_sb")
-                lo = lo_col(i)
-                if lo > 0:
-                    nc.gpsimd.memset(e_sb[:, :, 0:lo // 4, :], 0.0)
-                nc.scalar.activation(out=e_sb[:, :, lo // 4:, :],
-                                     in_=s_main[i % 3][:, lo:W].rearrange("p (w u e) -> p u w e", u=2, e=2),
+                hi = hi_col(i)
+                if hi < W:
+                    nc.gpsimd.memset(e_sb[:, :, hi // 4:, :], 0.0)
+                nc.scalar.activation(out=e_sb[:, :, 0:hi // 4, :],
+                                     in_=s_main[i % 3][:, 0:hi].rearrange("p (w u e) -> p u w e", u=2, e=2),
                                      func=ACTF.Exp, bias=nm[:], scale=SCALE, accum_out=dn[:, 0, qt:qt + 1])
                 state[("e", i)] = e_sb
             nc.scalar.activation(out=bstate[("ed", b)][:, :, qt, :, :],
@@ -286,13 +278,14 @@ def tile_baseattention_t_kernel(tc, q, k, v, out):
         def edge_regroup(b):
             nc.scalar.copy(out=grouped_words(b)[:, SUBS, :, :], in_=s_edge[b % 2][:, 0:2, :].rearrange("p u r -> p r u"))
 
-        def quant(b, x):
+        def quant(b, x0, x1):
             if ("w", b) not in bstate:
                 bstate[("w", b)] = (wp.tile([P, SUBS + 1, P], I32, name="e_words", align_bytes=64),
                                     wp.tile([P, SUBS + 1, P], U8, name="e_scales", align_bytes=64))
             e_words, e_scales = bstate[("w", b)]
-            nc.vector.quantize_mx(out=e_words[:, x, :].bitcast(FP8X4), scales=e_scales[:, x, :],
-                                  in_=bstate[("g", b)][:, x, :, :].rearrange("p r t -> p (r t)"))
+            nc.vector.quantize_mx(out=e_words[:, x0:x1, :].rearrange("p x r -> p (x r)").bitcast(FP8X4),
+                                  scales=e_scales[:, x0:x1, :].rearrange("p x r -> p (x r)"),
+                                  in_=bstate[("g", b)][:, x0:x1, :, :].rearrange("p x r t -> p (x r t)"))
 
         def mx(b):
             h, n = blocks[b]
@@ -300,8 +293,8 @@ def tile_baseattention_t_kernel(tc, q, k, v, out):
             for qt in range(SUBS):
                 ops = []
                 if has_main(b * SUBS + qt):
-                    ops.append((qt, v_own[(b - 1) % NVQ][:] if qt == 0 else v_mix[b % NVM][:, qt - 1, :]))
-                ops.append((SUBS, v_diag[b % NVM][:, qt, :]))
+                    ops.append((qt, v_own[(b - 1) % NVQ][:] if qt == 0 else v_spread[b % NVM][:, qt, :]))
+                ops.append((SUBS, v_spread[b % NVM][:, ALONE[qt], :]))
                 for x, vop in ops:
                     nc.tensor.matmul_mx(out=o_ps[:, qt, :], lhsT=e_words[:, x, :].bitcast(FP8X4),
                                         lhsT_scale=e_scales[:, x, :], rhs=codes(vop), rhs_scale=scales(vop),
@@ -344,9 +337,10 @@ def tile_baseattention_t_kernel(tc, q, k, v, out):
             if x is not None:
                 f(x, *args)
 
-        def quant_tile(i):
-            if has_main(i):
-                quant(i // SUBS, i % SUBS)
+        def quant_two(i):
+            h, n, qt = tiles[i]
+            if qt % 2 == 1:
+                quant(i // SUBS, qt - 1 if has_main(i - 1) else qt, qt + 1)
 
         def quant_and_spread_v(b):
             quant_v(b)
@@ -366,17 +360,17 @@ def tile_baseattention_t_kernel(tc, q, k, v, out):
             when(block_at(s, AT_MX), mx)
             when(block_at(s, AT_EDGE_MAX), edge_max)
             when(tile_at(s, AT_MAX), main_max)
-            when(tile_at(s, AT_QUANT), quant_tile)
-            when(block_at(s, AT_EDGE_QUANT), quant, SUBS)
+            when(block_at(s, AT_OUT), finish)
             if s == 0:
                 quant_and_spread_v(0)
             when(block_at(s, AT_V_QUANT, 1), quant_and_spread_v)
-            when(block_at(s, AT_OUT), finish)
+            when(tile_at(s, AT_QUANT), quant_two)
+            when(block_at(s, AT_EDGE_QUANT), quant, SUBS, SUBS + 1)
             when(block_at(s, AT_SUM), sum_up)
             when(tile_at(s, AT_MAX), combine)
             when(block_at(s, AT_RECIP), recip)
             when(tile_at(s, AT_EXP), exps)
-            when(block_at(s, AT_PREP_COPY, 1), prep_copy, o_bf)
             when(block_at(s, AT_EDGE_FLIP), edge_regroup)
+            when(block_at(s, AT_PREP, 1), prep_copy, o_bf)
             when(tile_at(s, AT_COPY), regroup)
             when(block_at(s, AT_V_GROUP, 2), group_v)

@@ -31,19 +31,19 @@ AT_MAX = 1
 AT_EXP = 2
 AT_FLIP = 4
 AT_COPY = 4
-AT_QUANT = 5
+AT_QUANT = 6
 AT_V_GROUP = -5
-AT_V_QUANT = -3
+AT_V_QUANT = -2
 AT_PREP = -3
 AT_EDGE = 0
 AT_EDGE_MAX = 1
 AT_EDGE_FLIP = 6
+AT_EDGE_COPY = 7
 AT_SUM = 6
-AT_RECIP = 7
+AT_RECIP = 9
 AT_EDGE_QUANT = 9
 AT_MX = 10
 AT_OUT = 11
-QT_VECTOR = 1
 ALONE = (0, 4, 5, 6)
 
 
@@ -73,17 +73,35 @@ def tile_baseattention_t_kernel(tc, q, k, v, out):
             k_raw.append(const.tile([P, NS, P], BF16, name="k_raw%d" % h))
             v_raw.append(const.tile([P, NB, 4, P], BF16, name="v_raw%d" % h))
 
-        def load(h, n0, n1):
-            a = n0 * SUBS
-            b = n1 * SUBS
+        def load_qk(h, a, b):
             nc.sync.dma_start(out=q_raw[h][:, a:b, :], in_=qv[:, h * NS + a:h * NS + b, :])
             nc.sync.dma_start(out=k_raw[h][:, a:b, :], in_=kv[:, h * NS + a:h * NS + b, :])
+
+        def load_v(h, n0, n1):
             nc.sync.dma_start(out=v_raw[h][:, n0:n1, :, :], in_=vv[:, h * NB + n0:h * NB + n1, :, :])
 
-        load(0, 0, 1)
-        load(0, 1, 2)
-        load(0, 2, 4)
-        load(0, 4, NB)
+        load_qk(0, 0, 1)
+        load_qk(0, 1, SUBS)
+        load_qk(0, SUBS, 2 * SUBS)
+        load_v(0, 0, 2)
+        for n0, n1 in ((2, 4), (4, NB)):
+            load_qk(0, n0 * SUBS, n1 * SUBS)
+            load_v(0, n0, n1)
+
+        v_own = []
+        v_spread = []
+        for j in range(NVQ):
+            t = const.tile([P, VW], I32, name="v_own%d" % j, align_bytes=64)
+            nc.vector.memset(t[:, P:VW], 0)
+            v_own.append(t)
+        for j in range(NVM):
+            t = const.tile([P, 7, VW], I32, name="v_spread%d" % j, align_bytes=64)
+            if j == 0:
+                nc.vector.memset(t[:], 0)
+            else:
+                nc.vector.memset(t[:, 0, :], 0)
+                nc.vector.memset(t[:, SUBS:, :], 0)
+            v_spread.append(t)
 
         ident = const.tile([P, P], BF16, name="ident")
         make_identity(nc, ident[:])
@@ -96,29 +114,28 @@ def tile_baseattention_t_kernel(tc, q, k, v, out):
         nc.gpsimd.affine_select(out=mask_f[:, 1, :], in_=mask_f[:, 1, :], compare_op=ALU.is_ge, fill=NEG,
                                 base=0, pattern=[[-1, P]], channel_multiplier=1)
         mask = const.tile([P, 1 + SUBS, P], BF16, name="mask")
-        for j in range(1 + SUBS):
+        for j in reversed(range(1 + SUBS)):
             nc.vector.tensor_copy(out=mask[:, j, :], in_=mask_f[:, min(j, 1), :])
 
         xT = []
         for h in range(H):
             xT.append(const.tile([P, 2, T], BF16, name="xT%d" % h))
-        v_own = []
-        v_spread = []
-        for j in range(NVQ):
-            t = const.tile([P, VW], I32, name="v_own%d" % j, align_bytes=64)
-            nc.vector.memset(t[:], 0)
-            v_own.append(t)
-        for j in range(NVM):
-            t = const.tile([P, 7, VW], I32, name="v_spread%d" % j, align_bytes=64)
-            nc.vector.memset(t[:], 0)
-            v_spread.append(t)
 
         s_main = [psum.tile([P, W], F32, name="s_main%d" % j) for j in range(3)]
         s_edge = [psum.tile([P, SUBS, P], F32, name="s_edge%d" % j) for j in range(2)]
-        flipped = [psum.tile([P, 4, P], F32, name="flipped%d" % j) for j in range(2)]
-        o_ps = psum.tile([P, SUBS, P], F32, name="o_ps")
-        o_bf = o_ps[:].rearrange("p j c -> p (j c)").bitcast(BF16).rearrange("p (j c) -> p j c", c=P)
-        flip_bf = flipped[0][:].rearrange("p j c -> p (j c)").bitcast(BF16).rearrange("p (j c) -> p j c", c=P)
+        turn = [psum.tile([P, SUBS, P], F32, name="turn%d" % j) for j in range(3)]
+        turns = []
+
+        def next_bank(use):
+            turns.append(use)
+            return bank_of(use)
+
+        def bank_of(use):
+            return turn[turns.index(use) % len(turn)]
+
+        def as_bf16(bank):
+            return bank[:].rearrange("p j c -> p (j c)").bitcast(BF16).rearrange("p (j c) -> p j c", c=P)
+
 
         tiles = [(h, n, qt) for h in range(H) for n in range(NB) for qt in range(SUBS)]
         blocks = [(h, n) for h in range(H) for n in range(NB)]
@@ -131,20 +148,26 @@ def tile_baseattention_t_kernel(tc, q, k, v, out):
             h, n, qt = tiles[i]
             return n > 0 or qt > 0
 
+        def diag_in_main(i):
+            return not has_main(i)
+
         def hi_col(i):
             h, n, qt = tiles[i]
-            return W if n > 0 else qt * P
+            return W if n > 0 else max(qt, 1) * P
 
-        def prep_pe(b, p_ps):
+        def prep_pe(b, j0=0, j1=SUBS):
             h, n = blocks[b]
-            for j in range(SUBS):
-                nc.tensor.transpose(p_ps[:, j, :], q_raw[h][:, n * SUBS + j, :], ident[:])
-            for j in range(SUBS):
-                nc.tensor.transpose(p_ps[:, SUBS + j, :], k_raw[h][:, n * SUBS + j, :], ident[:])
+            p_ps = as_bf16(next_bank(("qk", b, j0)))
+            for x, raw in enumerate((q_raw, k_raw)):
+                for j in range(j0, j1):
+                    nc.tensor.transpose(p_ps[:, x * SUBS + j, :], raw[h][:, n * SUBS + j, :], ident[:])
 
-        def prep_copy(b, p_ps):
+        def prep_copy(b, j0=0, j1=SUBS):
             h, n = blocks[b]
-            nc.scalar.copy(out=xT[h][:, :, n * W:(n + 1) * W], in_=p_ps.rearrange("p (a j) c -> p a (j c)", a=2))
+            p_ps = as_bf16(bank_of(("qk", b, j0)))
+            cols = slice((n * SUBS + j0) * P, (n * SUBS + j1) * P)
+            nc.scalar.copy(out=xT[h][:, :, cols].rearrange("p a (j c) -> p a j c", c=P),
+                           in_=p_ps.rearrange("p (a j) c -> p a j c", a=2)[:, :, j0:j1, :])
 
         def group_v(b):
             h, n = blocks[b]
@@ -185,16 +208,18 @@ def tile_baseattention_t_kernel(tc, q, k, v, out):
         def edge_pe(b):
             h, n = blocks[b]
             se = s_edge[b % 2]
-            nc.tensor.matmul(se[:].rearrange("p j c -> p (j c)"), lhsT=ident[:],
-                             rhs=mask[:, 1:, :].rearrange("p j c -> p (j c)"), start=True, stop=False)
-            for j in range(SUBS):
+            j0 = 1 if diag_in_main(b * SUBS) else 0
+            nc.tensor.matmul(se[:, j0:, :].rearrange("p j c -> p (j c)"), lhsT=ident[:],
+                             rhs=mask[:, 1 + j0:, :].rearrange("p j c -> p (j c)"), start=True, stop=False)
+            for j in range(j0, SUBS):
                 row = n * SUBS + j
                 nc.tensor.matmul(se[:, j, :], lhsT=xT[h][:, 0, row * P:(row + 1) * P],
                                  rhs=xT[h][:, 1, row * P:(row + 1) * P], start=False, stop=(j == SUBS - 1))
 
         def edge_max(b):
+            j0 = 1 if diag_in_main(b * SUBS) else 0
             m_edge = stat.tile([P, SUBS], F32, name="m_edge")
-            nc.vector.tensor_reduce(out=m_edge[:], in_=s_edge[b % 2][:], axis=AX.X, op=ALU.max)
+            nc.vector.tensor_reduce(out=m_edge[:, j0:], in_=s_edge[b % 2][:, j0:, :], axis=AX.X, op=ALU.max)
             dn = stat.tile([P, 2, SUBS], F32, name="dn")
             if blocks[b][1] == 0:
                 nc.gpsimd.memset(dn[:, 0, 0:1], 0.0)
@@ -213,17 +238,19 @@ def tile_baseattention_t_kernel(tc, q, k, v, out):
                 nc.tensor.matmul(sm[:, qt * P:(qt + 1) * P], lhsT=ident[:], rhs=mask[:, 0, :], start=False, stop=True)
             if qt > 0:
                 nc.tensor.matmul(sm[:, 0:qt * P], lhsT=qT, rhs=xT[h][:, 1, n * W:row * P], start=True, stop=True)
+            if diag_in_main(i):
+                nc.tensor.matmul(sm[:, 0:P], lhsT=ident[:], rhs=mask[:, 1, :], start=True, stop=False)
+                nc.tensor.matmul(sm[:, 0:P], lhsT=qT, rhs=xT[h][:, 1, row * P:(row + 1) * P], start=False, stop=True)
 
         def main_max(i):
-            if has_main(i):
-                m_main = stat.tile([P, 1], F32, name="m_main")
-                nc.vector.tensor_reduce(out=m_main[:], in_=s_main[i % 3][:, 0:hi_col(i)], axis=AX.X, op=ALU.max)
-                state[("mm", i)] = m_main
+            m_main = stat.tile([P, 1], F32, name="m_main")
+            nc.vector.tensor_reduce(out=m_main[:], in_=s_main[i % 3][:, 0:hi_col(i)], axis=AX.X, op=ALU.max)
+            state[("mm", i)] = m_main
 
         def combine(i):
             h, n, qt = tiles[i]
-            me = bstate[("me", i // SUBS)][:, qt:qt + 1]
-            m_main = state[("mm", i)][:] if has_main(i) else me
+            m_main = state[("mm", i)][:]
+            me = m_main if diag_in_main(i) else bstate[("me", i // SUBS)][:, qt:qt + 1]
             nm = stat.tile([P, 1], F32, name="nm")
             nc.vector.tensor_scalar(out=nm[:], in0=m_main, scalar1=me, scalar2=-SCALE, op0=ALU.max, op1=ALU.mult)
             state[("nm", i)] = nm
@@ -242,21 +269,24 @@ def tile_baseattention_t_kernel(tc, q, k, v, out):
                                      in_=s_main[i % 3][:, 0:hi].rearrange("p (w u e) -> p u w e", u=2, e=2),
                                      func=ACTF.Exp, bias=nm[:], scale=SCALE, accum_out=dn[:, 0, qt:qt + 1])
                 state[("e", i)] = e_sb
+            diag = s_main[i % 3][:, 0:P] if diag_in_main(i) else s_edge[b % 2][:, qt, :]
             nc.scalar.activation(out=bstate[("ed", b)][:, :, qt, :, :],
-                                 in_=s_edge[b % 2][:, qt, :].rearrange("p (w u e) -> p u w e", u=2, e=2),
+                                 in_=diag.rearrange("p (w u e) -> p u w e", u=2, e=2),
                                  func=ACTF.Exp, bias=nm[:], scale=SCALE, accum_out=dn[:, 1, qt:qt + 1])
 
-        def flip_pe(i):
-            if has_main(i):
-                words = state[("e", i)][:].rearrange("p u w e -> p (u w e)").bitcast(F32)
-                for u in range(2):
-                    nc.tensor.transpose(flipped[i // 2 % 2][:, 2 * (i % 2) + u, :], words[:, u * P:(u + 1) * P],
-                                        ident_f[:])
+        def flip_pe(m):
+            bank = next_bank(("e", m))
+            for i in (2 * m, 2 * m + 1):
+                if has_main(i):
+                    words = state[("e", i)][:].rearrange("p u w e -> p (u w e)").bitcast(F32)
+                    for u in range(2):
+                        nc.tensor.transpose(bank[:, 2 * (i % 2) + u, :], words[:, u * P:(u + 1) * P], ident_f[:])
 
         def edge_flip(b):
+            bank = next_bank(("diagonal", b))
             words = bstate[("ed", b)][:].rearrange("p u j w e -> p (u j w e)").bitcast(F32)
             for u in range(2):
-                nc.tensor.transpose(s_edge[b % 2][:, u, :], words[:, u * P:(u + 1) * P], ident_f[:])
+                nc.tensor.transpose(bank[:, u, :], words[:, u * P:(u + 1) * P], ident_f[:])
 
         def grouped_words(b):
             if ("g", b) not in bstate:
@@ -264,19 +294,18 @@ def tile_baseattention_t_kernel(tc, q, k, v, out):
             g = bstate[("g", b)]
             return g[:].rearrange("p x r t -> p (x r t)").bitcast(F32).rearrange("p (x r u) -> p x r u", r=P, u=2)
 
-        def regroup(i):
-            h, n, qt = tiles[i]
-            if has_main(i):
-                r0 = 2 * (i % 2)
-                src = flipped[i // 2 % 2][:, r0:r0 + 2, :].rearrange("p u r -> p r u")
-                dst = grouped_words(i // SUBS)[:, qt, :, :]
-                if qt == QT_VECTOR:
-                    nc.vector.tensor_copy(out=dst, in_=src)
-                else:
-                    nc.scalar.copy(out=dst, in_=src)
+        def places(m):
+            x0 = 2 * (m % 2)
+            return (x0 if has_main(2 * m) else x0 + 1), x0 + 2
+
+        def regroup(m):
+            x0, x1 = places(m)
+            src = bank_of(("e", m))[:, 2 * (x0 - x1):, :].rearrange("p (x u) r -> p x r u", u=2)
+            nc.scalar.copy(out=grouped_words(m // 2)[:, x0:x1, :, :], in_=src)
 
         def edge_regroup(b):
-            nc.scalar.copy(out=grouped_words(b)[:, SUBS, :, :], in_=s_edge[b % 2][:, 0:2, :].rearrange("p u r -> p r u"))
+            src = bank_of(("diagonal", b))[:, 0:2, :].rearrange("p u r -> p r u")
+            nc.scalar.copy(out=grouped_words(b)[:, SUBS, :, :], in_=src)
 
         def quant(b, x0, x1):
             if ("w", b) not in bstate:
@@ -290,13 +319,14 @@ def tile_baseattention_t_kernel(tc, q, k, v, out):
         def mx(b):
             h, n = blocks[b]
             e_words, e_scales = bstate[("w", b)]
+            bank = next_bank(("out", b))
             for qt in range(SUBS):
                 ops = []
                 if has_main(b * SUBS + qt):
                     ops.append((qt, v_own[(b - 1) % NVQ][:] if qt == 0 else v_spread[b % NVM][:, qt, :]))
                 ops.append((SUBS, v_spread[b % NVM][:, ALONE[qt], :]))
                 for x, vop in ops:
-                    nc.tensor.matmul_mx(out=o_ps[:, qt, :], lhsT=e_words[:, x, :].bitcast(FP8X4),
+                    nc.tensor.matmul_mx(out=bank[:, qt, :], lhsT=e_words[:, x, :].bitcast(FP8X4),
                                         lhsT_scale=e_scales[:, x, :], rhs=codes(vop), rhs_scale=scales(vop),
                                         start=(x == ops[0][0]), stop=(x == SUBS))
 
@@ -315,19 +345,24 @@ def tile_baseattention_t_kernel(tc, q, k, v, out):
             h, n = blocks[b]
             rd = bstate[("rd", b)]
             o_sb = op.tile([P, SUBS, P], F32, name="o_sb")
-            nc.vector.tensor_tensor(out=o_sb[:], in0=o_ps[:], in1=rd[:].unsqueeze(2).to_broadcast([P, SUBS, P]),
+            nc.vector.tensor_tensor(out=o_sb[:], in0=bank_of(("out", b))[:], in1=rd[:].unsqueeze(2).to_broadcast([P, SUBS, P]),
                                     op=ALU.mult)
             r0 = h * NS + n * SUBS
             nc.sync.dma_start(out=ov[:, r0:r0 + SUBS, :], in_=o_sb[:])
 
-        prep_pe(0, flip_bf)
-        prep_copy(0, flip_bf)
+        for j0, j1 in ((0, 1), (1, SUBS)):
+            prep_pe(0, j0, j1)
+            prep_copy(0, j0, j1)
+        main_pe(0)
+        edge_pe(0)
+        main_max(0)
+        combine(0)
+        edge_max(0)
         group_v(0)
-        prep_pe(1, o_bf)
         group_v(1)
 
-        def tile_at(s, at):
-            return s - at if 0 <= s - at < NT else None
+        def tile_at(s, at, first=0):
+            return s - at if first <= s - at < NT else None
 
         def block_at(s, at, first=0):
             b = (s - at) // SUBS
@@ -337,10 +372,11 @@ def tile_baseattention_t_kernel(tc, q, k, v, out):
             if x is not None:
                 f(x, *args)
 
-        def quant_two(i):
-            h, n, qt = tiles[i]
-            if qt % 2 == 1:
-                quant(i // SUBS, qt - 1 if has_main(i - 1) else qt, qt + 1)
+        def pair_at(s, at):
+            return (s - at) // 2 if (s - at) % 2 == 0 and 0 <= s - at < NT else None
+
+        def quant_two(m):
+            quant(m // 2, *places(m))
 
         def quant_and_spread_v(b):
             quant_v(b)
@@ -349,28 +385,28 @@ def tile_baseattention_t_kernel(tc, q, k, v, out):
         for s in range(NT + AT_OUT):
             if s % (NB * SUBS) in (4, 12) and s // (NB * SUBS) + 1 < H:
                 half = 0 if s % (NB * SUBS) == 4 else NB // 2
-                load(s // (NB * SUBS) + 1, half, half + NB // 2)
-            when(block_at(s, AT_EDGE), edge_pe)
-            if (s - AT_FLIP) % 2 == 0:
-                when(tile_at(s, AT_FLIP), flip_pe)
-                when(tile_at(s, AT_FLIP - 1), flip_pe)
-            when(block_at(s, AT_EDGE_FLIP), edge_flip)
-            when(block_at(s, AT_PREP, 2), prep_pe, o_bf)
-            when(tile_at(s, 0), main_pe)
+                load_qk(s // (NB * SUBS) + 1, half * SUBS, (half + NB // 2) * SUBS)
+                load_v(s // (NB * SUBS) + 1, half, half + NB // 2)
+            prep = 1 if s == AT_PREP + SUBS + 1 else block_at(s, AT_PREP, 2)
+            when(block_at(s, AT_EDGE, 1), edge_pe)
+            when(prep, prep_pe)
+            when(pair_at(s, AT_FLIP), flip_pe)
+            when(tile_at(s, 0, 1), main_pe)
             when(block_at(s, AT_MX), mx)
-            when(block_at(s, AT_EDGE_MAX), edge_max)
-            when(tile_at(s, AT_MAX), main_max)
-            when(block_at(s, AT_OUT), finish)
-            if s == 0:
-                quant_and_spread_v(0)
-            when(block_at(s, AT_V_QUANT, 1), quant_and_spread_v)
-            when(tile_at(s, AT_QUANT), quant_two)
-            when(block_at(s, AT_EDGE_QUANT), quant, SUBS, SUBS + 1)
+            when(block_at(s, AT_EDGE_FLIP), edge_flip)
+            when(block_at(s, AT_EDGE_MAX, 1), edge_max)
+            when(tile_at(s, AT_MAX, 1), main_max)
+            if s in (3, 4):
+                quant_and_spread_v(s - 3)
+            when(block_at(s, AT_V_QUANT, 2), quant_and_spread_v)
+            when(pair_at(s, AT_QUANT), quant_two)
             when(block_at(s, AT_SUM), sum_up)
-            when(tile_at(s, AT_MAX), combine)
+            when(tile_at(s, AT_MAX, 1), combine)
+            when(block_at(s, AT_EDGE_QUANT), quant, SUBS, SUBS + 1)
+            when(block_at(s, AT_OUT), finish)
             when(block_at(s, AT_RECIP), recip)
             when(tile_at(s, AT_EXP), exps)
-            when(block_at(s, AT_EDGE_FLIP), edge_regroup)
-            when(block_at(s, AT_PREP, 1), prep_copy, o_bf)
-            when(tile_at(s, AT_COPY), regroup)
+            when(block_at(s, AT_EDGE_COPY), edge_regroup)
+            when(prep, prep_copy)
+            when(pair_at(s, AT_COPY), regroup)
             when(block_at(s, AT_V_GROUP, 2), group_v)

@@ -30,20 +30,21 @@ NVM = 5
 AT_MAX = 1
 AT_EXP = 2
 AT_FLIP = 4
-AT_COPY = 4
-AT_QUANT = 6
+AT_COPY = 5
+AT_QUANT = 8
 AT_V_GROUP = -5
-AT_V_QUANT = -2
+AT_V_QUANT = -3
 AT_PREP = -3
+AT_PREP_COPY = -2
 AT_EDGE = 0
 AT_EDGE_MAX = 1
-AT_EDGE_FLIP = 6
-AT_EDGE_COPY = 7
-AT_SUM = 6
-AT_RECIP = 9
-AT_EDGE_QUANT = 9
-AT_MX = 10
-AT_OUT = 11
+AT_SUM = 7
+AT_EDGE_FLIP = 7
+AT_EDGE_COPY = 9
+AT_EDGE_QUANT = 10
+AT_RECIP = 10
+AT_MX = 11
+AT_OUT = 12
 ALONE = (0, 4, 5, 6)
 
 
@@ -305,7 +306,7 @@ def tile_baseattention_t_kernel(tc, q, k, v, out):
 
         def edge_regroup(b):
             src = bank_of(("diagonal", b))[:, 0:2, :].rearrange("p u r -> p r u")
-            nc.scalar.copy(out=grouped_words(b)[:, SUBS, :, :], in_=src)
+            nc.vector.tensor_copy(out=grouped_words(b)[:, SUBS, :, :], in_=src)
 
         def quant(b, x0, x1):
             if ("w", b) not in bstate:
@@ -375,6 +376,9 @@ def tile_baseattention_t_kernel(tc, q, k, v, out):
         def pair_at(s, at):
             return (s - at) // 2 if (s - at) % 2 == 0 and 0 <= s - at < NT else None
 
+        def prep_at(s, at):
+            return 1 if s == at + SUBS + 1 else block_at(s, at, 2)
+
         def quant_two(m):
             quant(m // 2, *places(m))
 
@@ -387,12 +391,11 @@ def tile_baseattention_t_kernel(tc, q, k, v, out):
                 half = 0 if s % (NB * SUBS) == 4 else NB // 2
                 load_qk(s // (NB * SUBS) + 1, half * SUBS, (half + NB // 2) * SUBS)
                 load_v(s // (NB * SUBS) + 1, half, half + NB // 2)
-            prep = 1 if s == AT_PREP + SUBS + 1 else block_at(s, AT_PREP, 2)
             when(block_at(s, AT_EDGE, 1), edge_pe)
-            when(prep, prep_pe)
-            when(pair_at(s, AT_FLIP), flip_pe)
             when(tile_at(s, 0, 1), main_pe)
             when(block_at(s, AT_MX), mx)
+            when(pair_at(s, AT_FLIP), flip_pe)
+            when(prep_at(s, AT_PREP), prep_pe)
             when(block_at(s, AT_EDGE_FLIP), edge_flip)
             when(block_at(s, AT_EDGE_MAX, 1), edge_max)
             when(tile_at(s, AT_MAX, 1), main_max)
@@ -403,10 +406,10 @@ def tile_baseattention_t_kernel(tc, q, k, v, out):
             when(block_at(s, AT_SUM), sum_up)
             when(tile_at(s, AT_MAX, 1), combine)
             when(block_at(s, AT_EDGE_QUANT), quant, SUBS, SUBS + 1)
+            when(block_at(s, AT_EDGE_COPY), edge_regroup)
             when(block_at(s, AT_OUT), finish)
             when(block_at(s, AT_RECIP), recip)
             when(tile_at(s, AT_EXP), exps)
-            when(block_at(s, AT_EDGE_COPY), edge_regroup)
-            when(prep, prep_copy)
+            when(prep_at(s, AT_PREP_COPY), prep_copy)
             when(pair_at(s, AT_COPY), regroup)
             when(block_at(s, AT_V_GROUP, 2), group_v)

@@ -31,20 +31,20 @@ AT_MAX = 1
 AT_EXP = 2
 AT_FLIP = 4
 AT_COPY = 5
-AT_QUANT = 8
+AT_QUANT = 7
 AT_V_GROUP = -5
 AT_V_QUANT = -3
-AT_PREP = -3
-AT_PREP_COPY = -2
+AT_PREP = -4
+AT_PREP_COPY = -3
 AT_EDGE = 0
-AT_EDGE_MAX = 1
+AT_EDGE_MAX = 0
 AT_SUM = 7
 AT_EDGE_FLIP = 7
-AT_EDGE_COPY = 9
-AT_EDGE_QUANT = 10
-AT_RECIP = 10
-AT_MX = 11
-AT_OUT = 12
+AT_EDGE_COPY = 8
+AT_EDGE_QUANT = 11
+AT_RECIP = 11
+AT_MX = 14
+AT_OUT = 14
 ALONE = (0, 4, 5, 6)
 
 
@@ -391,25 +391,25 @@ def tile_baseattention_t_kernel(tc, q, k, v, out):
                 half = 0 if s % (NB * SUBS) == 4 else NB // 2
                 load_qk(s // (NB * SUBS) + 1, half * SUBS, (half + NB // 2) * SUBS)
                 load_v(s // (NB * SUBS) + 1, half, half + NB // 2)
-            when(block_at(s, AT_EDGE, 1), edge_pe)
-            when(tile_at(s, 0, 1), main_pe)
-            when(block_at(s, AT_MX), mx)
-            when(pair_at(s, AT_FLIP), flip_pe)
-            when(prep_at(s, AT_PREP), prep_pe)
             when(block_at(s, AT_EDGE_FLIP), edge_flip)
-            when(block_at(s, AT_EDGE_MAX, 1), edge_max)
+            when(block_at(s, AT_MX), mx)
+            when(block_at(s, AT_EDGE, 1), edge_pe)
+            when(prep_at(s, AT_PREP), prep_pe)
+            when(tile_at(s, 0, 1), main_pe)
+            when(pair_at(s, AT_FLIP), flip_pe)
             when(tile_at(s, AT_MAX, 1), main_max)
+            when(block_at(s, AT_EDGE_MAX, 1), edge_max)
+            when(pair_at(s, AT_QUANT), quant_two)
             if s in (3, 4):
                 quant_and_spread_v(s - 3)
             when(block_at(s, AT_V_QUANT, 2), quant_and_spread_v)
-            when(pair_at(s, AT_QUANT), quant_two)
-            when(block_at(s, AT_SUM), sum_up)
-            when(tile_at(s, AT_MAX, 1), combine)
-            when(block_at(s, AT_EDGE_QUANT), quant, SUBS, SUBS + 1)
-            when(block_at(s, AT_EDGE_COPY), edge_regroup)
             when(block_at(s, AT_OUT), finish)
+            when(block_at(s, AT_EDGE_QUANT), quant, SUBS, SUBS + 1)
             when(block_at(s, AT_RECIP), recip)
-            when(tile_at(s, AT_EXP), exps)
+            when(block_at(s, AT_SUM), sum_up)
+            when(block_at(s, AT_EDGE_COPY), edge_regroup)
+            when(tile_at(s, AT_MAX, 1), combine)
             when(prep_at(s, AT_PREP_COPY), prep_copy)
+            when(tile_at(s, AT_EXP), exps)
             when(pair_at(s, AT_COPY), regroup)
             when(block_at(s, AT_V_GROUP, 2), group_v)

from contextlib import ExitStack

import concourse.mybir as mybir
from concourse.masks import make_identity

F32 = mybir.dt.float32
BF16 = mybir.dt.bfloat16
I32 = mybir.dt.int32
U8 = mybir.dt.uint8
FP8X4 = mybir.dt.float8_e4m3fn_x4
ALU = mybir.AluOpType
ACTF = mybir.ActivationFunctionType
AX = mybir.AxisListType

P = 128
H = 4
T = 4096
W = 512
NB = T // W
SUBS = W // P
NS = T // P
Q = P // SUBS
SCALE = 128.0 ** -0.5
NEG = -(2.0 ** 80)
FLOPS = 2 * (2 * NB - 1) * H * 2 * W * W * P
VW = P + P // 4
NVQ = 6
NVM = 5

AT_MAX = 1
AT_EXP = 2
AT_FLIP = 4
AT_COPY = 5
AT_QUANT = 7
AT_V_GROUP = -5
AT_V_QUANT = -3
AT_PREP = -4
AT_PREP_COPY = -3
AT_EDGE = 0
AT_EDGE_MAX = 0
AT_SUM = 7
AT_EDGE_FLIP = 7
AT_EDGE_COPY = 8
AT_EDGE_QUANT = 11
AT_RECIP = 11
AT_MX = 14
AT_OUT = 14
ALONE = (0, 4, 5, 6)


def tile_baseattention_t_kernel(tc, q, k, v, out):
    nc = tc.nc
    qv = q.rearrange("b h (s p) d -> p (b h s) d", p=P)
    kv = k.rearrange("b h (s p) d -> p (b h s) d", p=P)
    vv = v.rearrange("b h (n p t) d -> p (b h n) t d", p=P, t=4)
    ov = out.rearrange("b h (s p) d -> p (b h s) d", p=P)

    with ExitStack() as ctx:
        const = ctx.enter_context(tc.tile_pool(name="const", bufs=1))
        stat = ctx.enter_context(tc.tile_pool(name="stat", bufs=4))
        ep = ctx.enter_context(tc.tile_pool(name="ep", bufs=4))
        gp = ctx.enter_context(tc.tile_pool(name="gp", bufs=3))
        wp = ctx.enter_context(tc.tile_pool(name="wp", bufs=3))
        vgp = ctx.enter_context(tc.tile_pool(name="vgp", bufs=2))
        op = ctx.enter_context(tc.tile_pool(name="op", bufs=4))
        psum = ctx.enter_context(tc.psum_pool(name="psum", bufs=1))
        ctx.enter_context(tc.manual_schedule())

        q_raw = []
        k_raw = []
        v_raw = []
        for h in range(H):
            q_raw.append(const.tile([P, NS, P], BF16, name="q_raw%d" % h))
            k_raw.append(const.tile([P, NS, P], BF16, name="k_raw%d" % h))
            v_raw.append(const.tile([P, NB, 4, P], BF16, name="v_raw%d" % h))

        def load_qk(h, a, b):
            nc.sync.dma_start(out=q_raw[h][:, a:b, :], in_=qv[:, h * NS + a:h * NS + b, :])
            nc.sync.dma_start(out=k_raw[h][:, a:b, :], in_=kv[:, h * NS + a:h * NS + b, :])

        def load_v(h, n0, n1):
            nc.sync.dma_start(out=v_raw[h][:, n0:n1, :, :], in_=vv[:, h * NB + n0:h * NB + n1, :, :])

        load_qk(0, 0, 1)
        load_qk(0, 1, SUBS)
        load_qk(0, SUBS, 2 * SUBS)
        load_v(0, 0, 2)
        for n0, n1 in ((2, 4), (4, NB)):
            load_qk(0, n0 * SUBS, n1 * SUBS)
            load_v(0, n0, n1)

        v_own = []
        v_spread = []
        for j in range(NVQ):
            t = const.tile([P, VW], I32, name="v_own%d" % j, align_bytes=64)
            nc.vector.memset(t[:, P:VW], 0)
            v_own.append(t)
        for j in range(NVM):
            t = const.tile([P, 7, VW], I32, name="v_spread%d" % j, align_bytes=64)
            if j == 0:
                nc.vector.memset(t[:], 0)
            else:
                nc.vector.memset(t[:, 0, :], 0)
                nc.vector.memset(t[:, SUBS:, :], 0)
            v_spread.append(t)

        ident = const.tile([P, P], BF16, name="ident")
        make_identity(nc, ident[:])
        ident_f = const.tile([P, P], F32, name="ident_f")
        make_identity(nc, ident_f[:])
        mask_f = const.tile([P, 2, P], F32, name="mask_f")
        nc.gpsimd.memset(mask_f[:], 0.0)
        nc.gpsimd.affine_select(out=mask_f[:, 0, :], in_=mask_f[:, 0, :], compare_op=ALU.is_ge, fill=NEG,
                                base=-1, pattern=[[1, P]], channel_multiplier=-1)
        nc.gpsimd.affine_select(out=mask_f[:, 1, :], in_=mask_f[:, 1, :], compare_op=ALU.is_ge, fill=NEG,
                                base=0, pattern=[[-1, P]], channel_multiplier=1)
        mask = const.tile([P, 1 + SUBS, P], BF16, name="mask")
        for j in reversed(range(1 + SUBS)):
            nc.vector.tensor_copy(out=mask[:, j, :], in_=mask_f[:, min(j, 1), :])

        xT = []
        for h in range(H):
            xT.append(const.tile([P, 2, T], BF16, name="xT%d" % h))

        s_main = [psum.tile([P, W], F32, name="s_main%d" % j) for j in range(3)]
        s_edge = [psum.tile([P, SUBS, P], F32, name="s_edge%d" % j) for j in range(2)]
        turn = [psum.tile([P, SUBS, P], F32, name="turn%d" % j) for j in range(3)]
        turns = []

        def next_bank(use):
            turns.append(use)
            return bank_of(use)

        def bank_of(use):
            return turn[turns.index(use) % len(turn)]

        def as_bf16(bank):
            return bank[:].rearrange("p j c -> p (j c)").bitcast(BF16).rearrange("p (j c) -> p j c", c=P)


        tiles = [(h, n, qt) for h in range(H) for n in range(NB) for qt in range(SUBS)]
        blocks = [(h, n) for h in range(H) for n in range(NB)]
        NT = len(tiles)
        NBLK = len(blocks)
        state = {}
        bstate = {}

        def has_main(i):
            h, n, qt = tiles[i]
            return n > 0 or qt > 0

        def diag_in_main(i):
            return not has_main(i)

        def hi_col(i):
            h, n, qt = tiles[i]
            return W if n > 0 else max(qt, 1) * P

        def prep_pe(b, j0=0, j1=SUBS):
            h, n = blocks[b]
            p_ps = as_bf16(next_bank(("qk", b, j0)))
            for x, raw in enumerate((q_raw, k_raw)):
                for j in range(j0, j1):
                    nc.tensor.transpose(p_ps[:, x * SUBS + j, :], raw[h][:, n * SUBS + j, :], ident[:])

        def prep_copy(b, j0=0, j1=SUBS):
            h, n = blocks[b]
            p_ps = as_bf16(bank_of(("qk", b, j0)))
            cols = slice((n * SUBS + j0) * P, (n * SUBS + j1) * P)
            nc.scalar.copy(out=xT[h][:, :, cols].rearrange("p a (j c) -> p a j c", c=P),
                           in_=p_ps.rearrange("p (a j) c -> p a j c", a=2)[:, :, j0:j1, :])

        def group_v(b):
            h, n = blocks[b]
            v_g = vgp.tile([P, P, 4], BF16, name="v_g", align_bytes=64)
            nc.gpsimd.tensor_scalar(out=v_g[:], in0=v_raw[h][:, n, :, :].rearrange("p t d -> p d t"),
                                    scalar1=1.0, scalar2=0.0, op0=ALU.mult, op1=ALU.add)
            bstate[("vg", b)] = v_g

        def codes(ap):
            return ap[:, 0:P].bitcast(FP8X4)

        def scales(ap):
            return ap[:, P:VW].bitcast(U8)

        def quant_v(b):
            own = v_own[b % NVQ]
            nc.vector.quantize_mx(out=codes(own), scales=scales(own),
                                  in_=bstate[("vg", b)][:].rearrange("p d t -> p (d t)"))

        def spread_v(b):
            h, n = blocks[b]
            own = v_own[b % NVQ]
            prev = v_own[(b - 1) % NVQ]

            def put(src, j, slots, cnt):
                rows = slice(j * Q, (j + 1) * Q)
                nc.sync.dma_start(out=v_spread[b % NVM][rows, slots, :],
                                  in_=src[rows, :].unsqueeze(1).to_broadcast([Q, cnt, VW]))

            put(own, 0, slice(0, 4), 4)
            put(own, 1, slice(2, 5), 3)
            put(own, 2, slice(3, 6, 2), 2)
            put(own, 3, slice(6, 7), 1)
            if n > 0:
                for j in range(1, SUBS):
                    put(prev, j, slice(1, j + 1), j)

        def edge_pe(b):
            h, n = blocks[b]
            se = s_edge[b % 2]
            j0 = 1 if diag_in_main(b * SUBS) else 0
            nc.tensor.matmul(se[:, j0:, :].rearrange("p j c -> p (j c)"), lhsT=ident[:],
                             rhs=mask[:, 1 + j0:, :].rearrange("p j c -> p (j c)"), start=True, stop=False)
            for j in range(j0, SUBS):
                row = n * SUBS + j
                nc.tensor.matmul(se[:, j, :], lhsT=xT[h][:, 0, row * P:(row + 1) * P],
                                 rhs=xT[h][:, 1, row * P:(row + 1) * P], start=False, stop=(j == SUBS - 1))

        def edge_max(b):
            j0 = 1 if diag_in_main(b * SUBS) else 0
            m_edge = stat.tile([P, SUBS], F32, name="m_edge")
            nc.vector.tensor_reduce(out=m_edge[:, j0:], in_=s_edge[b % 2][:, j0:, :], axis=AX.X, op=ALU.max)
            dn = stat.tile([P, 2, SUBS], F32, name="dn")
            if blocks[b][1] == 0:
                nc.gpsimd.memset(dn[:, 0, 0:1], 0.0)
            e_diag = ep.tile([P, 2, SUBS, Q, 2], BF16, name="e_diag")
            bstate[("me", b)] = m_edge
            bstate[("dn", b)] = dn
            bstate[("ed", b)] = e_diag

        def main_pe(i):
            h, n, qt = tiles[i]
            sm = s_main[i % 3]
            row = n * SUBS + qt
            qT = xT[h][:, 0, row * P:(row + 1) * P]
            if n > 0:
                nc.tensor.matmul(sm[:, qt * P:W], lhsT=qT, rhs=xT[h][:, 1, row * P - W:n * W], start=True, stop=False)
                nc.tensor.matmul(sm[:, qt * P:(qt + 1) * P], lhsT=ident[:], rhs=mask[:, 0, :], start=False, stop=True)
            if qt > 0:
                nc.tensor.matmul(sm[:, 0:qt * P], lhsT=qT, rhs=xT[h][:, 1, n * W:row * P], start=True, stop=True)
            if diag_in_main(i):
                nc.tensor.matmul(sm[:, 0:P], lhsT=ident[:], rhs=mask[:, 1, :], start=True, stop=False)
                nc.tensor.matmul(sm[:, 0:P], lhsT=qT, rhs=xT[h][:, 1, row * P:(row + 1) * P], start=False, stop=True)

        def main_max(i):
            m_main = stat.tile([P, 1], F32, name="m_main")
            nc.vector.tensor_reduce(out=m_main[:], in_=s_main[i % 3][:, 0:hi_col(i)], axis=AX.X, op=ALU.max)
            state[("mm", i)] = m_main

        def combine(i):
            h, n, qt = tiles[i]
            m_main = state[("mm", i)][:]
            me = m_main if diag_in_main(i) else bstate[("me", i // SUBS)][:, qt:qt + 1]
            nm = stat.tile([P, 1], F32, name="nm")
            nc.vector.tensor_scalar(out=nm[:], in0=m_main, scalar1=me, scalar2=-SCALE, op0=ALU.max, op1=ALU.mult)
            state[("nm", i)] = nm

        def exps(i):
            h, n, qt = tiles[i]
            b = i // SUBS
            nm = state[("nm", i)]
            dn = bstate[("dn", b)]
            if has_main(i):
                e_sb = ep.tile([P, 2, P, 2], BF16, name="e_sb")
                hi = hi_col(i)
                if hi < W:
                    nc.gpsimd.memset(e_sb[:, :, hi // 4:, :], 0.0)
                nc.scalar.activation(out=e_sb[:, :, 0:hi // 4, :],
                                     in_=s_main[i % 3][:, 0:hi].rearrange("p (w u e) -> p u w e", u=2, e=2),
                                     func=ACTF.Exp, bias=nm[:], scale=SCALE, accum_out=dn[:, 0, qt:qt + 1])
                state[("e", i)] = e_sb
            diag = s_main[i % 3][:, 0:P] if diag_in_main(i) else s_edge[b % 2][:, qt, :]
            nc.scalar.activation(out=bstate[("ed", b)][:, :, qt, :, :],
                                 in_=diag.rearrange("p (w u e) -> p u w e", u=2, e=2),
                                 func=ACTF.Exp, bias=nm[:], scale=SCALE, accum_out=dn[:, 1, qt:qt + 1])

        def flip_pe(m):
            bank = next_bank(("e", m))
            for i in (2 * m, 2 * m + 1):
                if has_main(i):
                    words = state[("e", i)][:].rearrange("p u w e -> p (u w e)").bitcast(F32)
                    for u in range(2):
                        nc.tensor.transpose(bank[:, 2 * (i % 2) + u, :], words[:, u * P:(u + 1) * P], ident_f[:])

        def edge_flip(b):
            bank = next_bank(("diagonal", b))
            words = bstate[("ed", b)][:].rearrange("p u j w e -> p (u j w e)").bitcast(F32)
            for u in range(2):
                nc.tensor.transpose(bank[:, u, :], words[:, u * P:(u + 1) * P], ident_f[:])

        def grouped_words(b):
            if ("g", b) not in bstate:
                bstate[("g", b)] = gp.tile([P, SUBS + 1, P, 4], BF16, name="grouped", align_bytes=64)
            g = bstate[("g", b)]
            return g[:].rearrange("p x r t -> p (x r t)").bitcast(F32).rearrange("p (x r u) -> p x r u", r=P, u=2)

        def places(m):
            x0 = 2 * (m % 2)
            return (x0 if has_main(2 * m) else x0 + 1), x0 + 2

        def regroup(m):
            x0, x1 = places(m)
            src = bank_of(("e", m))[:, 2 * (x0 - x1):, :].rearrange("p (x u) r -> p x r u", u=2)
            nc.scalar.copy(out=grouped_words(m // 2)[:, x0:x1, :, :], in_=src)

        def edge_regroup(b):
            src = bank_of(("diagonal", b))[:, 0:2, :].rearrange("p u r -> p r u")
            nc.vector.tensor_copy(out=grouped_words(b)[:, SUBS, :, :], in_=src)

        def quant(b, x0, x1):
            if ("w", b) not in bstate:
                bstate[("w", b)] = (wp.tile([P, SUBS + 1, P], I32, name="e_words", align_bytes=64),
                                    wp.tile([P, SUBS + 1, P], U8, name="e_scales", align_bytes=64))
            e_words, e_scales = bstate[("w", b)]
            nc.vector.quantize_mx(out=e_words[:, x0:x1, :].rearrange("p x r -> p (x r)").bitcast(FP8X4),
                                  scales=e_scales[:, x0:x1, :].rearrange("p x r -> p (x r)"),
                                  in_=bstate[("g", b)][:, x0:x1, :, :].rearrange("p x r t -> p (x r t)"))

        def mx(b):
            h, n = blocks[b]
            e_words, e_scales = bstate[("w", b)]
            bank = next_bank(("out", b))
            for qt in range(SUBS):
                ops = []
                if has_main(b * SUBS + qt):
                    ops.append((qt, v_own[(b - 1) % NVQ][:] if qt == 0 else v_spread[b % NVM][:, qt, :]))
                ops.append((SUBS, v_spread[b % NVM][:, ALONE[qt], :]))
                for x, vop in ops:
                    nc.tensor.matmul_mx(out=bank[:, qt, :], lhsT=e_words[:, x, :].bitcast(FP8X4),
                                        lhsT_scale=e_scales[:, x, :], rhs=codes(vop), rhs_scale=scales(vop),
                                        start=(x == ops[0][0]), stop=(x == SUBS))

        def sum_up(b):
            dn = bstate[("dn", b)]
            ds = stat.tile([P, SUBS], F32, name="ds")
            nc.vector.tensor_tensor(out=ds[:], in0=dn[:, 0, :], in1=dn[:, 1, :], op=ALU.add)
            bstate[("ds", b)] = ds

        def recip(b):
            rd = stat.tile([P, SUBS], F32, name="rd")
            nc.vector.reciprocal(out=rd[:], in_=bstate[("ds", b)][:])
            bstate[("rd", b)] = rd

        def finish(b):
            h, n = blocks[b]
            rd = bstate[("rd", b)]
            o_sb = op.tile([P, SUBS, P], F32, name="o_sb")
            nc.vector.tensor_tensor(out=o_sb[:], in0=bank_of(("out", b))[:], in1=rd[:].unsqueeze(2).to_broadcast([P, SUBS, P]),
                                    op=ALU.mult)
            r0 = h * NS + n * SUBS
            nc.sync.dma_start(out=ov[:, r0:r0 + SUBS, :], in_=o_sb[:])

        for j0, j1 in ((0, 1), (1, SUBS)):
            prep_pe(0, j0, j1)
            prep_copy(0, j0, j1)
        main_pe(0)
        edge_pe(0)
        main_max(0)
        combine(0)
        edge_max(0)
        group_v(0)
        group_v(1)

        def tile_at(s, at, first=0):
            return s - at if first <= s - at < NT else None

        def block_at(s, at, first=0):
            b = (s - at) // SUBS
            return b if (s - at) % SUBS == 0 and first <= b < NBLK else None

        def when(x, f, *args):
            if x is not None:
                f(x, *args)

        def pair_at(s, at):
            return (s - at) // 2 if (s - at) % 2 == 0 and 0 <= s - at < NT else None

        def prep_at(s, at):
            return 1 if s == at + SUBS + 1 else block_at(s, at, 2)

        def quant_two(m):
            quant(m // 2, *places(m))

        def quant_and_spread_v(b):
            quant_v(b)
            spread_v(b)

        for s in range(NT + AT_OUT):
            if s % (NB * SUBS) in (4, 12) and s // (NB * SUBS) + 1 < H:
                half = 0 if s % (NB * SUBS) == 4 else NB // 2
                load_qk(s // (NB * SUBS) + 1, half * SUBS, (half + NB // 2) * SUBS)
                load_v(s // (NB * SUBS) + 1, half, half + NB // 2)
            when(block_at(s, AT_EDGE_FLIP), edge_flip)
            when(block_at(s, AT_MX), mx)
            when(block_at(s, AT_EDGE, 1), edge_pe)
            when(prep_at(s, AT_PREP), prep_pe)
            when(tile_at(s, 0, 1), main_pe)
            when(pair_at(s, AT_FLIP), flip_pe)
            when(tile_at(s, AT_MAX, 1), main_max)
            when(block_at(s, AT_EDGE_MAX, 1), edge_max)
            when(pair_at(s, AT_QUANT), quant_two)
            if s in (3, 4):
                quant_and_spread_v(s - 3)
            when(block_at(s, AT_V_QUANT, 2), quant_and_spread_v)
            when(block_at(s, AT_OUT), finish)
            when(block_at(s, AT_EDGE_QUANT), quant, SUBS, SUBS + 1)
            when(block_at(s, AT_RECIP), recip)
            when(block_at(s, AT_SUM), sum_up)
            when(block_at(s, AT_EDGE_COPY), edge_regroup)
            when(tile_at(s, AT_MAX, 1), combine)
            when(prep_at(s, AT_PREP_COPY), prep_copy)
            when(tile_at(s, AT_EXP), exps)
            when(pair_at(s, AT_COPY), regroup)
            when(block_at(s, AT_V_GROUP, 2), group_v)
